import numpy as np
import ml_dtypes


def mxq(x, axis, fmt="e4m3"):
    dtype, down = {"e4m3": (ml_dtypes.float8_e4m3fn, 7), "e5m2": (ml_dtypes.float8_e5m2, 14)}[fmt]
    v = np.moveaxis(np.asarray(x, np.float32).astype(ml_dtypes.bfloat16).astype(np.float64), axis, -1)
    blocks = v.reshape(v.shape[:-1] + (-1, 32))
    amax = np.abs(blocks).max(-1, keepdims=True)
    byte = np.maximum(np.where(amax > 0, np.frexp(amax)[1] - 1 + 127, 0) - down, 1)
    scale = np.exp2(byte - 127.0)
    codes = (blocks / scale).astype(np.float32).astype(dtype).astype(np.float64)
    return np.moveaxis((codes * scale).reshape(v.shape), -1, axis)


WIDE = False


def mx_kscale(k):
    if not WIDE:
        return np.ones(k)
    levels = np.array([30, -30])
    if k % 512:
        return np.exp2(np.random.permutation(np.resize(levels, k // 32))).repeat(32)
    a = np.empty((k // 512, 16))
    for p in range(k // 512):
        a[p, :8] = np.random.permutation(np.resize(levels, 8))
        for g in range(8):
            far = levels[np.abs(levels - a[p, g]) >= 10]
            a[p, g + 8] = far[np.random.randint(len(far))]
    return np.exp2(a.ravel()).repeat(32)


BF16 = ml_dtypes.bfloat16


def bf(x):
    return np.asarray(x, np.float32).astype(BF16)


def f64(x):
    return np.asarray(x).astype(np.float64)


E2M1 = np.array([0.0, 0.5, 1.0, 1.5, 2.0, 3.0, 4.0, 6.0, -0.0, -0.5, -1.0, -1.5, -2.0, -3.0, -4.0, -6.0])


def pack_weight(w, fmt):
    k, n = w.shape
    w = f64(bf(w)).reshape(k // 32, 32, n)
    amax = np.abs(w).max(1)
    if fmt == "e4m3":
        byte = np.frexp(amax)[1] - 1 + 127 - 7
    else:
        mant, ex = np.frexp(amax / 6.0)
        byte = np.where(mant > 0.5, ex, ex - 1) + 127
    byte = np.clip(np.where(amax > 0, byte, 1), 1, 254)
    scaled = (w * np.exp2(127.0 - byte)[:, None, :]).reshape(k, n).astype(np.float32)
    by_word = np.ascontiguousarray(scaled.reshape(k // 512, 128, 4, n).transpose(0, 1, 3, 2))
    if fmt == "e4m3":
        words = by_word.astype(ml_dtypes.float8_e4m3fn).view(np.uint8)
    else:
        c = by_word.astype(ml_dtypes.float4_e2m1fn).view(np.uint8) & 0xF
        words = c[..., 0::2] | (c[..., 1::2] << 4)
    return np.ascontiguousarray(words), np.ascontiguousarray(byte.astype(np.uint8).reshape(k // 512, 16, n))


def unpack_weight(words, scales, fmt):
    g, p, n, _ = words.shape
    if fmt == "e4m3":
        vals = np.ascontiguousarray(words).view(ml_dtypes.float8_e4m3fn).astype(np.float64)
    else:
        nib = np.empty((g, p, n, 4), np.uint8)
        nib[..., 0::2] = words & 0xF
        nib[..., 1::2] = words >> 4
        vals = E2M1[nib]
    vals = vals * np.repeat(np.exp2(scales.astype(np.float64) - 127.0), 8, axis=1)[..., None]
    return vals.transpose(0, 1, 3, 2).reshape(g * 512, n)

def pack4(w):
    words, scales = pack_weight(w, "e2m1")
    return words.reshape(words.shape[0], 128, -1), scales


def unpack4(words, scales):
    return unpack_weight(words.reshape(words.shape[0], 128, -1, 2), scales, "e2m1")


B, C, T, H = 4, 1536, 512, 512
EPS_LN = 1e-5
EPS_STD = 1e-5


def ln_dim1(z, g, b):
    mu = z.mean(axis=1, keepdims=True)
    var = ((z - mu) ** 2).mean(axis=1, keepdims=True)
    return (z - mu) / np.sqrt(var + EPS_LN) * g[None, :, None] + b[None, :, None]


def stats(x, m):
    mean = (m * x).sum(axis=2)
    std = np.sqrt(np.maximum((m * x * x).sum(axis=2) - mean ** 2, EPS_STD))
    return mean, std


def setup_inputs():
    s = mx_kscale(H)
    drop = np.random.randint(B, size=T)
    mask = (np.arange(B)[:, None, None] != drop[None, None, :]) * 1.0
    off = 0.5 * np.random.standard_normal((B, C, 1))
    gain = 0.5 + np.random.random((B, C, 1))
    pad = np.random.standard_normal((B, C, 1)) * (1.0 - mask)
    x = off + gain * np.random.standard_normal((B, C, T)) + pad
    h = bf(np.tanh(np.random.standard_normal((B, H, T))) * s[None, :, None])
    w2 = np.random.standard_normal((C, H)) * 3.0 / np.sqrt(H) / s[None, :]
    w2_words, w2_scales = pack4(np.ascontiguousarray(w2.T))
    return {"h": h,
            "x": bf(x),
            "mask": bf(mask),
            "w2_words": w2_words,
            "w2_scales": w2_scales,
            "b2": bf(0.1 * np.random.standard_normal(C)),
            "g2": bf(1.0 + 0.1 * np.random.standard_normal(2 * C)),
            "be2": bf(0.1 * np.random.standard_normal(2 * C))}


def reference(h, x, mask, w2_words, w2_scales, b2, g2, be2):
    x, mask = f64(x), f64(mask)
    alpha = (unpack4(w2_words, w2_scales).T @ mxq(f64(h), 1, "e5m2")) + f64(b2)[None, :, None]
    alpha = np.where(mask == 0, -np.inf, alpha)
    e = np.exp(alpha - alpha.max(axis=2, keepdims=True))
    alpha = e / e.sum(axis=2, keepdims=True)
    mean, std = stats(x, alpha)
    out = np.concatenate([mean, std], axis=1)[:, :, None]
    return ln_dim1(out, f64(g2), f64(be2))

@@ -1,0 +1,283 @@
+from contextlib import ExitStack
+
+import concourse.mybir as mybir
+from concourse.masks import make_identity
+
+B, C, T, H = 4, 1536, 512, 512
+FLOPS = 2 * B * C * H * T
+
+F32 = mybir.dt.float32
+BF16 = mybir.dt.bfloat16
+U32 = mybir.dt.uint32
+U8 = mybir.dt.uint8
+I32 = mybir.dt.int32
+E5M2X4 = mybir.dt.float8_e5m2_x4
+E2M1X4 = mybir.dt.float4_e2m1fn_x4
+ACT = mybir.ActivationFunctionType
+ALU = mybir.AluOpType
+AX = mybir.AxisListType
+
+P = 128
+NCB = C // 512
+NG = B * NCB
+NT = NG * 4
+JT = C // P
+BIG = 2.0 ** 100
+EPS_STD = 1e-5
+EPS_LN = 1e-5
+
+
+def tile_attentivestatspool_pb_kernel(tc, h, x, mask, w2_words, w2_scales, b2, g2, be2, out):
+    nc = tc.nc
+    with ExitStack() as ctx:
+        const = ctx.enter_context(tc.tile_pool(name="const", bufs=1))
+        hilp = ctx.enter_context(tc.tile_pool(name="hilp", bufs=2))
+        namp = ctx.enter_context(tc.tile_pool(name="namp", bufs=3))
+        ep = ctx.enter_context(tc.tile_pool(name="ep", bufs=4))
+        pp = ctx.enter_context(tc.tile_pool(name="pp", bufs=2))
+        psa = ctx.enter_context(tc.psum_pool(name="psa", bufs=3))
+        psb = ctx.enter_context(tc.psum_pool(name="psb", bufs=4))
+        psm = ctx.enter_context(tc.psum_pool(name="psm", bufs=1))
+        ctx.enter_context(tc.manual_schedule())
+
+        hraw = []
+        for b in range(B):
+            hr = const.tile([P, 4, T], BF16, name="hraw%d" % b)
+            hraw.append(hr)
+        codes = []
+        hsc = []
+        for b in range(B):
+            cd = const.tile([P, T], U32, name="codes%d" % b, align_bytes=64)
+            sc = const.tile([P, T], U8, name="hsc%d" % b, align_bytes=64)
+            codes.append(cd)
+            hsc.append(sc)
+        xs = []
+        for g in range(NG):
+            xt = const.tile([P, 4, T], BF16, name="x%d" % g)
+            xs.append(xt)
+        wwords = const.tile([P, 2 * C], U8, name="wwords", align_bytes=64)
+        wplane = const.tile([P, C], U8, name="wplane", align_bytes=64)
+        mrow = const.tile([P, P], BF16, name="mrow")
+        pbrow = const.tile([P, P], F32, name="pbrow")
+        pb = const.tile([P, 16], F32, name="pb")
+        ident = const.tile([P, P], F32, name="ident")
+        ones = const.tile([P, P], F32, name="ones")
+        warm = const.tile([P, 1], F32, name="warm")
+        warm2 = const.tile([P, 1], F32, name="warm2")
+        s0 = const.tile([P, NT], F32, name="s0")
+        s1 = const.tile([P, NT], F32, name="s1")
+        s2 = const.tile([P, NT], F32, name="s2")
+        negm = const.tile([P, NT], F32, name="negm")
+        vt = const.tile([P, 2 * NT], F32, name="vt")
+        vn = const.tile([P, P], F32, name="vn")
+        g2t = const.tile([P, P], BF16, name="g2t")
+        be2t = const.tile([P, P], BF16, name="be2t")
+
+        def load_h(b):
+            nc.sync.dma_start(out=hraw[b][:], in_=h[b].rearrange("(p j) t -> p j t", j=4))
+
+        def load_x(g):
+            b, cb = divmod(g, NCB)
+            nc.sync.dma_start(
+                out=xs[g][:],
+                in_=x[b, cb * 512 : (cb + 1) * 512, :].rearrange("(cc p) t -> p cc t", p=P),
+            )
+
+        load_h(0)
+        nc.vector.memset(mrow[:], 0.0)
+        nc.vector.memset(wplane[:].bitcast(I32), 0)
+        nc.sync.dma_start(out=mrow[0:16, :], in_=mask.rearrange("b o (tb p) -> (b o tb) p", p=P))
+        for q in range(4):
+            nc.sync.dma_start(
+                out=wplane[32 * q : 32 * q + 4, :].bitcast(I32),
+                in_=w2_scales[0, 4 * q : 4 * q + 4, :].bitcast(I32),
+            )
+        nc.sync.dma_start(out=wwords[:].bitcast(I32), in_=w2_words[0].bitcast(I32))
+        load_h(1)
+        load_x(0)
+        load_x(1)
+        load_x(2)
+        for b in range(1, B):
+            for cb in range(NCB):
+                load_x(b * NCB + cb)
+            if b + 1 < B:
+                load_h(b + 1)
+        for b in range(B):
+            nc.sync.dma_start(out=g2t[b * 24 : (b + 1) * 24, :], in_=g2.rearrange("(j p) -> j p", p=P))
+            nc.sync.dma_start(out=be2t[b * 24 : (b + 1) * 24, :], in_=be2.rearrange("(j p) -> j p", p=P))
+
+        nc.gpsimd.memset(warm[:], 1.0)
+        make_identity(nc, ident[:])
+        nc.gpsimd.memset(ones[:], 1.0)
+        nc.gpsimd.memset(vn[:], 0.0)
+        nc.scalar.activation(out=warm2[:], in_=warm[:], func=ACT.Exp)
+
+        nc.vector.tensor_scalar(out=pbrow[:], in0=mrow[:], scalar1=-BIG, scalar2=BIG, op0=ALU.mult, op1=ALU.add)
+        pbt = psm.tile([P, P], F32, name="pbt", tag="misc")
+        nc.tensor.transpose(pbt[:], pbrow[:], ident[:])
+        nc.vector.tensor_copy(out=pb[:], in_=pbt[:, 0:16])
+
+        hil = {}
+
+        def interleave(b, k, eng):
+            if k == 0:
+                hl = hilp.tile([P, T, 4], BF16, name="hil", align_bytes=64)
+                hil[b] = hl
+            dst = hil[b][:, k * P : (k + 1) * P, :]
+            src = hraw[b][:, :, k * P : (k + 1) * P].rearrange("p j t -> p t j")
+            if eng == "v":
+                nc.vector.tensor_copy(out=dst, in_=src)
+            else:
+                nc.scalar.copy(out=dst, in_=src)
+
+        def quantize(b):
+            nc.vector.quantize_mx(
+                out=codes[b][:].bitcast(E5M2X4),
+                scales=hsc[b][:],
+                in_=hil[b][:].rearrange("p t j -> p (t j)"),
+            )
+
+        interleave(0, 0, "v")
+        interleave(0, 1, "v")
+        interleave(0, 2, "v")
+        interleave(0, 3, "s")
+        quantize(0)
+
+        pa = {}
+        nam = {}
+        pbk = {}
+        et = {}
+
+        def mx(j):
+            g, tb = divmod(j, 4)
+            b, cb = divmod(g, NCB)
+            a = psa.tile([P, 512], F32, name="psA")
+            pa[j] = a
+            nc.tensor.matmul_mx(
+                out=a[:],
+                lhsT=codes[b][:, tb * P : (tb + 1) * P].bitcast(E5M2X4),
+                lhsT_scale=hsc[b][:, tb * P : (tb + 1) * P],
+                rhs=wwords[:, cb * 1024 : (cb + 1) * 1024].bitcast(E2M1X4),
+                rhs_scale=wplane[:, cb * 512 : (cb + 1) * 512],
+                start=True,
+                stop=True,
+            )
+
+        def ev(j):
+            g, tb = divmod(j, 4)
+            b = g // NCB
+            if tb == 0:
+                nt = namp.tile([P, 4, 512], F32, name="nam")
+                nam[g] = nt
+            col = b * 4 + tb
+            if j < 8 and j % 2 == 1:
+                nc.vector.tensor_scalar(
+                    out=nam[g][:, tb, :], in0=pa[j][:], scalar1=-1.0, scalar2=pb[:, col : col + 1],
+                    op0=ALU.mult, op1=ALU.add,
+                )
+            else:
+                nc.scalar.activation(
+                    out=nam[g][:, tb, :], in_=pa[j][:], func=ACT.Identity, bias=pb[:, col : col + 1], scale=-1.0
+                )
+
+        def tr(i):
+            g, cc = divmod(i, 4)
+            bk = psb.tile([P, 512], F32, name="psB")
+            pbk[i] = bk
+            for tb in range(4):
+                nc.tensor.transpose(bk[:, tb * P : (tb + 1) * P], nam[g][:, tb, cc * P : (cc + 1) * P], ident[:])
+
+        def mn(i):
+            nc.vector.tensor_reduce(out=negm[:, i : i + 1], in_=pbk[i][:], axis=AX.X, op=ALU.min)
+
+        def ex(i):
+            e = ep.tile([P, 512], F32, name="e")
+            et[i] = e
+            nc.scalar.activation(
+                out=e[:], in_=pbk[i][:], func=ACT.Exp, bias=negm[:, i : i + 1], scale=-1.0,
+                accum_out=s0[:, i : i + 1],
+            )
+
+        def prod(i):
+            g, cc = divmod(i, 4)
+            p1 = pp.tile([P, 512], F32, name="p1")
+            nc.vector.scalar_tensor_tensor(
+                out=p1[:], in0=et[i][:], scalar=1.0, in1=xs[g][:, cc, :], op0=ALU.mult, op1=ALU.mult,
+                accum_out=s1[:, i : i + 1],
+            )
+            p2 = pp.tile([P, 512], F32, name="p2")
+            nc.vector.scalar_tensor_tensor(
+                out=p2[:], in0=p1[:], scalar=1.0, in1=xs[g][:, cc, :], op0=ALU.mult, op1=ALU.mult,
+                accum_out=s2[:, i : i + 1],
+            )
+
+        for s in range(-9, NT):
+            if 0 <= s + 4 < NT:
+                tr(s + 4)
+            if s + 9 < NT:
+                mx(s + 9)
+            if 0 <= s + 8 < NT:
+                ev(s + 8)
+            for b in range(1, B):
+                k = s - (12 * b - 14)
+                if 0 <= k < 4:
+                    interleave(b, k, "s")
+            if 0 <= s + 2 < NT:
+                mn(s + 2)
+                ex(s + 2)
+                if s + 2 == NT - 1:
+                    nc.scalar.activation(out=warm2[:], in_=warm[:], func=ACT.Sqrt)
+            for b in range(1, B):
+                if s == 12 * b - 10:
+                    quantize(b)
+            if s >= 0:
+                prod(s)
+
+        def v3(ap, n):
+            return ap.rearrange("p (b j) -> p b j", b=B)[:, :, 0:n]
+
+        vt3 = vt[:].rearrange("p (b j) -> p b j", b=B)
+        r0 = const.tile([P, NT], F32, name="r0")
+        ex2 = const.tile([P, NT], F32, name="ex2")
+        msq = const.tile([P, NT], F32, name="msq")
+        t2 = const.tile([P, NT], F32, name="t2")
+        var = const.tile([P, NT], F32, name="var")
+        st = const.tile([P, 8], F32, name="st")
+        mom = const.tile([P, 8], F32, name="mom")
+        musq = const.tile([P, 4], F32, name="musq")
+        vle = const.tile([P, 4], F32, name="vle")
+        sd = const.tile([P, 4], F32, name="sd")
+        rstd = const.tile([P, 4], F32, name="rstd")
+        o1 = const.tile([P, P], F32, name="o1")
+        o2 = const.tile([P, P], F32, name="o2")
+
+        nc.vector.reciprocal(out=r0[:], in_=s0[:])
+        nc.vector.tensor_tensor(out=vt3[:, :, 0:JT], in0=v3(s1[:], JT), in1=v3(r0[:], JT), op=ALU.mult)
+        nc.vector.tensor_tensor(out=ex2[:], in0=s2[:], in1=r0[:], op=ALU.mult)
+        nc.vector.tensor_tensor(out=v3(msq[:], JT), in0=vt3[:, :, 0:JT], in1=vt3[:, :, 0:JT], op=ALU.mult)
+        nc.vector.scalar_tensor_tensor(
+            out=t2[:], in0=msq[:], scalar=EPS_STD, in1=ex2[:], op0=ALU.add, op1=ALU.max
+        )
+        nc.vector.tensor_tensor(out=var[:], in0=t2[:], in1=msq[:], op=ALU.subtract)
+        nc.scalar.activation(out=vt3[:, :, JT : 2 * JT], in_=v3(var[:], JT), func=ACT.Sqrt)
+        nc.vector.tensor_reduce(out=st[:, 4:8], in_=v3(t2[:], JT), axis=AX.X, op=ALU.add)
+        nc.vector.tensor_reduce(out=st[:, 0:4], in_=vt3, axis=AX.X, op=ALU.add)
+        tot = psm.tile([P, 8], F32, name="tot", tag="misc")
+        nc.tensor.matmul(out=tot[:], lhsT=ones[:], rhs=st[:], start=True, stop=True)
+        nc.vector.tensor_scalar(out=mom[:], in0=tot[:], scalar1=1.0 / (2 * C), scalar2=None, op0=ALU.mult)
+        nc.vector.tensor_tensor(out=musq[:], in0=mom[:, 0:4], in1=mom[:, 0:4], op=ALU.mult)
+        nc.vector.scalar_tensor_tensor(
+            out=vle[:], in0=mom[:, 4:8], scalar=EPS_LN, in1=musq[:], op0=ALU.add, op1=ALU.subtract
+        )
+        nc.scalar.activation(out=sd[:], in_=vle[:], func=ACT.Sqrt)
+        nc.vector.reciprocal(out=rstd[:], in_=sd[:])
+        for b in range(B):
+            nc.vector.tensor_scalar(
+                out=vn[:, b * 24 : (b + 1) * 24], in0=vt[:, b * 24 : (b + 1) * 24],
+                scalar1=mom[:, b : b + 1], scalar2=rstd[:, b : b + 1], op0=ALU.subtract, op1=ALU.mult,
+            )
+        vnt = psm.tile([P, P], F32, name="vnt", tag="misc")
+        nc.tensor.transpose(vnt[:], vn[:], ident[:])
+        nc.vector.tensor_tensor(out=o1[0:96, :], in0=vnt[0:96, :], in1=g2t[0:96, :], op=ALU.mult)
+        nc.vector.tensor_tensor(out=o2[0:96, :], in0=o1[0:96, :], in1=be2t[0:96, :], op=ALU.add)
+        nc.sync.dma_start(out=out.rearrange("b (j p) o -> (b j) (p o)", p=P), in_=o2[0:96, :])

@@ -22,6 +22,7 @@ NCB = C // 512
 NG = B * NCB
 NT = NG * 4
 JT = C // P
+NR = NT // 3
 BIG = 2.0 ** 100
 EPS_STD = 1e-5
 EPS_LN = 1e-5
@@ -33,22 +34,22 @@ def tile_attentivestatspool_pb_kernel(tc, h, x, mask, w2_words, w2_scales, b2, g
         const = ctx.enter_context(tc.tile_pool(name="const", bufs=1))
         hilp = ctx.enter_context(tc.tile_pool(name="hilp", bufs=2))
         namp = ctx.enter_context(tc.tile_pool(name="namp", bufs=3))
-        ep = ctx.enter_context(tc.tile_pool(name="ep", bufs=4))
-        pp = ctx.enter_context(tc.tile_pool(name="pp", bufs=2))
+        ep = ctx.enter_context(tc.tile_pool(name="ep", bufs=7))
+        pp = ctx.enter_context(tc.tile_pool(name="pp", bufs=3))
+        gp = ctx.enter_context(tc.tile_pool(name="gp", bufs=1))
         psa = ctx.enter_context(tc.psum_pool(name="psa", bufs=3))
         psb = ctx.enter_context(tc.psum_pool(name="psb", bufs=4))
         psm = ctx.enter_context(tc.psum_pool(name="psm", bufs=1))
         ctx.enter_context(tc.manual_schedule())
 
         hraw = []
-        for b in range(B):
-            hr = const.tile([P, 4, T], BF16, name="hraw%d" % b)
-            hraw.append(hr)
         codes = []
         hsc = []
         for b in range(B):
+            hr = const.tile([P, 4, T], BF16, name="hraw%d" % b)
             cd = const.tile([P, T], U32, name="codes%d" % b, align_bytes=64)
             sc = const.tile([P, T], U8, name="hsc%d" % b, align_bytes=64)
+            hraw.append(hr)
             codes.append(cd)
             hsc.append(sc)
         xs = []
@@ -61,15 +62,15 @@ def tile_attentivestatspool_pb_kernel(tc, h, x, mask, w2_words, w2_scales, b2, g
         pbrow = const.tile([P, P], F32, name="pbrow")
         pb = const.tile([P, 16], F32, name="pb")
         ident = const.tile([P, P], F32, name="ident")
-        ones = const.tile([P, P], F32, name="ones")
+        sel = const.tile([P, B, P], F32, name="sel")
         warm = const.tile([P, 1], F32, name="warm")
         warm2 = const.tile([P, 1], F32, name="warm2")
+        epst = const.tile([P, 1], F32, name="epst")
         s0 = const.tile([P, NT], F32, name="s0")
         s1 = const.tile([P, NT], F32, name="s1")
         s2 = const.tile([P, NT], F32, name="s2")
         negm = const.tile([P, NT], F32, name="negm")
-        vt = const.tile([P, 2 * NT], F32, name="vt")
-        vn = const.tile([P, P], F32, name="vn")
+        vt = const.tile([P, P], F32, name="vt")
         g2t = const.tile([P, P], BF16, name="g2t")
         be2t = const.tile([P, P], BF16, name="be2t")
 
@@ -84,9 +85,9 @@ def tile_attentivestatspool_pb_kernel(tc, h, x, mask, w2_words, w2_scales, b2, g
             )
 
         load_h(0)
-        nc.vector.memset(mrow[:], 0.0)
+        nc.gpsimd.memset(mrow[:], 0.0)
+        nc.scalar.dma_start(out=mrow[0:16, :], in_=mask.rearrange("b o (tb p) -> (b o tb) p", p=P))
         nc.vector.memset(wplane[:].bitcast(I32), 0)
-        nc.sync.dma_start(out=mrow[0:16, :], in_=mask.rearrange("b o (tb p) -> (b o tb) p", p=P))
         for q in range(4):
             nc.sync.dma_start(
                 out=wplane[32 * q : 32 * q + 4, :].bitcast(I32),
@@ -94,35 +95,38 @@ def tile_attentivestatspool_pb_kernel(tc, h, x, mask, w2_words, w2_scales, b2, g
             )
         nc.sync.dma_start(out=wwords[:].bitcast(I32), in_=w2_words[0].bitcast(I32))
         load_h(1)
-        load_x(0)
-        load_x(1)
-        load_x(2)
+        for cb in range(NCB):
+            load_x(cb)
         for b in range(1, B):
-            for cb in range(NCB):
-                load_x(b * NCB + cb)
             if b + 1 < B:
                 load_h(b + 1)
+            for cb in range(NCB):
+                load_x(b * NCB + cb)
         for b in range(B):
             nc.sync.dma_start(out=g2t[b * 24 : (b + 1) * 24, :], in_=g2.rearrange("(j p) -> j p", p=P))
             nc.sync.dma_start(out=be2t[b * 24 : (b + 1) * 24, :], in_=be2.rearrange("(j p) -> j p", p=P))
 
         nc.gpsimd.memset(warm[:], 1.0)
         make_identity(nc, ident[:])
-        nc.gpsimd.memset(ones[:], 1.0)
-        nc.gpsimd.memset(vn[:], 0.0)
         nc.scalar.activation(out=warm2[:], in_=warm[:], func=ACT.Exp)
+        nc.gpsimd.memset(vt[:], 0.0)
+        nc.gpsimd.memset(epst[:], EPS_LN)
+        nc.gpsimd.memset(sel[:], 0.0)
+        for b in range(B):
+            nc.gpsimd.memset(sel[:, b, 24 * b : 24 * (b + 1)], 1.0)
 
-        nc.vector.tensor_scalar(out=pbrow[:], in0=mrow[:], scalar1=-BIG, scalar2=BIG, op0=ALU.mult, op1=ALU.add)
-        pbt = psm.tile([P, P], F32, name="pbt", tag="misc")
-        nc.tensor.transpose(pbt[:], pbrow[:], ident[:])
-        nc.vector.tensor_copy(out=pb[:], in_=pbt[:, 0:16])
+        nc.gpsimd.tensor_scalar(out=pbrow[:], in0=mrow[:], scalar1=-BIG, scalar2=BIG, op0=ALU.mult, op1=ALU.add)
+        pbt = psm.tile([P, 512], F32, name="pbt", tag="misc")
+        nc.tensor.transpose(pbt[:, 0:P], pbrow[:], ident[:])
+        nc.scalar.copy(out=pb[:], in_=pbt[:, 0:16])
 
         hil = {}
 
+        def new_hil(b):
+            hl = hilp.tile([P, T, 4], BF16, name="hil", align_bytes=64)
+            hil[b] = hl
+
         def interleave(b, k, eng):
-            if k == 0:
-                hl = hilp.tile([P, T, 4], BF16, name="hil", align_bytes=64)
-                hil[b] = hl
             dst = hil[b][:, k * P : (k + 1) * P, :]
             src = hraw[b][:, :, k * P : (k + 1) * P].rearrange("p j t -> p t j")
             if eng == "v":
@@ -130,25 +134,35 @@ def tile_attentivestatspool_pb_kernel(tc, h, x, mask, w2_words, w2_scales, b2, g
             else:
                 nc.scalar.copy(out=dst, in_=src)
 
-        def quantize(b):
+        def quantize(b, lo, hi):
             nc.vector.quantize_mx(
-                out=codes[b][:].bitcast(E5M2X4),
-                scales=hsc[b][:],
-                in_=hil[b][:].rearrange("p t j -> p (t j)"),
+                out=codes[b][:, lo:hi].bitcast(E5M2X4),
+                scales=hsc[b][:, lo:hi],
+                in_=hil[b][:, lo:hi, :].rearrange("p t j -> p (t j)"),
             )
 
+        new_hil(0)
         interleave(0, 0, "v")
         interleave(0, 1, "v")
-        interleave(0, 2, "v")
+        interleave(0, 2, "s")
         interleave(0, 3, "s")
-        quantize(0)
+        for k in range(4):
+            quantize(0, k * P, (k + 1) * P)
+        new_hil(1)
+        nc.gpsimd.tensor_scalar(
+            out=hil[1][:], in0=hraw[1][:].rearrange("p j t -> p t j"), scalar1=1.0, scalar2=0.0,
+            op0=ALU.mult, op1=ALU.add,
+        )
 
         pa = {}
         nam = {}
         pbk = {}
         et = {}
+        pt = {}
 
         def mx(j):
+            if not 0 <= j < NT:
+                return
             g, tb = divmod(j, 4)
             b, cb = divmod(g, NCB)
             a = psa.tile([P, 512], F32, name="psA")
@@ -164,13 +178,15 @@ def tile_attentivestatspool_pb_kernel(tc, h, x, mask, w2_words, w2_scales, b2, g
             )
 
         def ev(j):
+            if not 0 <= j < NT:
+                return
             g, tb = divmod(j, 4)
             b = g // NCB
             if tb == 0:
                 nt = namp.tile([P, 4, 512], F32, name="nam")
                 nam[g] = nt
             col = b * 4 + tb
-            if j < 8 and j % 2 == 1:
+            if j in (1, 3):
                 nc.vector.tensor_scalar(
                     out=nam[g][:, tb, :], in0=pa[j][:], scalar1=-1.0, scalar2=pb[:, col : col + 1],
                     op0=ALU.mult, op1=ALU.add,
@@ -181,6 +197,8 @@ def tile_attentivestatspool_pb_kernel(tc, h, x, mask, w2_words, w2_scales, b2, g
                 )
 
         def tr(i):
+            if not 0 <= i < NT:
+                return
             g, cc = divmod(i, 4)
             bk = psb.tile([P, 512], F32, name="psB")
             pbk[i] = bk
@@ -188,96 +206,140 @@ def tile_attentivestatspool_pb_kernel(tc, h, x, mask, w2_words, w2_scales, b2, g
                 nc.tensor.transpose(bk[:, tb * P : (tb + 1) * P], nam[g][:, tb, cc * P : (cc + 1) * P], ident[:])
 
         def mn(i):
+            if not 0 <= i < NT:
+                return
             nc.vector.tensor_reduce(out=negm[:, i : i + 1], in_=pbk[i][:], axis=AX.X, op=ALU.min)
 
         def ex(i):
+            if not 0 <= i < NT:
+                return
             e = ep.tile([P, 512], F32, name="e")
             et[i] = e
             nc.scalar.activation(
                 out=e[:], in_=pbk[i][:], func=ACT.Exp, bias=negm[:, i : i + 1], scale=-1.0,
                 accum_out=s0[:, i : i + 1],
             )
+            if i == NT - 1:
+                nc.scalar.activation(out=warm2[:], in_=warm[:], func=ACT.Sqrt)
 
-        def prod(i):
+        def xtile(i):
             g, cc = divmod(i, 4)
+            return xs[g][:, cc, :]
+
+        def prod1(i):
             p1 = pp.tile([P, 512], F32, name="p1")
+            pt[i] = p1
             nc.vector.scalar_tensor_tensor(
-                out=p1[:], in0=et[i][:], scalar=1.0, in1=xs[g][:, cc, :], op0=ALU.mult, op1=ALU.mult,
+                out=p1[:], in0=et[i][:], scalar=1.0, in1=xtile(i), op0=ALU.mult, op1=ALU.mult,
                 accum_out=s1[:, i : i + 1],
             )
+
+        def prod1_gpsimd(i):
+            pg = gp.tile([P, 512], F32, name="pg")
+            pt[i] = pg
+            nc.gpsimd.tensor_tensor(out=pg[:], in0=et[i][:], in1=xtile(i), op=ALU.mult)
+
+        def sum1_scalar(i):
+            sj = gp.tile([P, 512], BF16, name="sj")
+            nc.scalar.activation(out=sj[:], in_=pt[i][:], func=ACT.Identity, accum_out=s1[:, i : i + 1])
+
+        def prod2(i):
             p2 = pp.tile([P, 512], F32, name="p2")
             nc.vector.scalar_tensor_tensor(
-                out=p2[:], in0=p1[:], scalar=1.0, in1=xs[g][:, cc, :], op0=ALU.mult, op1=ALU.mult,
+                out=p2[:], in0=pt[i][:], scalar=1.0, in1=xtile(i), op0=ALU.mult, op1=ALU.mult,
                 accum_out=s2[:, i : i + 1],
             )
 
-        for s in range(-9, NT):
-            if 0 <= s + 4 < NT:
-                tr(s + 4)
-            if s + 9 < NT:
-                mx(s + 9)
-            if 0 <= s + 8 < NT:
-                ev(s + 8)
-            for b in range(1, B):
-                k = s - (12 * b - 14)
+        for v in range(-4, NR):
+            a = 3 * v
+            na = a + 3
+            ta = a + 6
+            j0 = a + 9
+            helped = 0 <= v < NR - 1
+            ev(j0)
+            ev(j0 + 1)
+            mn(na)
+            mn(na + 1)
+            mn(na + 2)
+            if helped:
+                prod1_gpsimd(a)
+            ex(na)
+            ev(j0 + 2)
+            tr(ta)
+            tr(ta + 1)
+            ex(na + 1)
+            tr(ta + 2)
+            if helped:
+                sum1_scalar(a)
+            ex(na + 2)
+            for b in range(2, B):
+                k = v - (4 * b - 8)
                 if 0 <= k < 4:
+                    if k == 0:
+                        new_hil(b)
                     interleave(b, k, "s")
-            if 0 <= s + 2 < NT:
-                mn(s + 2)
-                ex(s + 2)
-                if s + 2 == NT - 1:
-                    nc.scalar.activation(out=warm2[:], in_=warm[:], func=ACT.Sqrt)
-            for b in range(1, B):
-                if s == 12 * b - 10:
-                    quantize(b)
-            if s >= 0:
-                prod(s)
+            if v >= 0:
+                if not helped:
+                    prod1(a)
+                prod1(a + 1)
+                prod1(a + 2)
+                prod2(a + 1)
+                prod2(a + 2)
+                for b in range(1, B):
+                    if v == 4 * b - 4:
+                        quantize(b, 0, T)
+                prod2(a)
+            mx(j0 + 3)
+            mx(j0 + 4)
+            mx(j0 + 5)
 
-        def v3(ap, n):
-            return ap.rearrange("p (b j) -> p b j", b=B)[:, :, 0:n]
+        def v3(ap):
+            return ap.rearrange("p (b j) -> p b j", b=B)
 
-        vt3 = vt[:].rearrange("p (b j) -> p b j", b=B)
+        vt3 = v3(vt[:, 0 : 2 * NT])
         r0 = const.tile([P, NT], F32, name="r0")
         ex2 = const.tile([P, NT], F32, name="ex2")
         msq = const.tile([P, NT], F32, name="msq")
         t2 = const.tile([P, NT], F32, name="t2")
         var = const.tile([P, NT], F32, name="var")
-        st = const.tile([P, 8], F32, name="st")
-        mom = const.tile([P, 8], F32, name="mom")
-        musq = const.tile([P, 4], F32, name="musq")
-        vle = const.tile([P, 4], F32, name="vle")
-        sd = const.tile([P, 4], F32, name="sd")
-        rstd = const.tile([P, 4], F32, name="rstd")
+        st = const.tile([P, 2 * B], F32, name="st")
+        mom = const.tile([P, 2], F32, name="mom")
+        nv = const.tile([P, 1], F32, name="nv")
+        sd = const.tile([P, 1], F32, name="sd")
+        rstd = const.tile([P, 1], F32, name="rstd")
         o1 = const.tile([P, P], F32, name="o1")
         o2 = const.tile([P, P], F32, name="o2")
+        st3 = st[:].rearrange("p (b k) -> p k b", k=2)
+        R = 2 * JT * B
 
         nc.vector.reciprocal(out=r0[:], in_=s0[:])
-        nc.vector.tensor_tensor(out=vt3[:, :, 0:JT], in0=v3(s1[:], JT), in1=v3(r0[:], JT), op=ALU.mult)
+        nc.vector.tensor_tensor(out=vt3[:, :, 0:JT], in0=v3(s1[:]), in1=v3(r0[:]), op=ALU.mult)
         nc.vector.tensor_tensor(out=ex2[:], in0=s2[:], in1=r0[:], op=ALU.mult)
-        nc.vector.tensor_tensor(out=v3(msq[:], JT), in0=vt3[:, :, 0:JT], in1=vt3[:, :, 0:JT], op=ALU.mult)
+        nc.vector.tensor_tensor(out=v3(msq[:]), in0=vt3[:, :, 0:JT], in1=vt3[:, :, 0:JT], op=ALU.mult)
         nc.vector.scalar_tensor_tensor(
             out=t2[:], in0=msq[:], scalar=EPS_STD, in1=ex2[:], op0=ALU.add, op1=ALU.max
         )
         nc.vector.tensor_tensor(out=var[:], in0=t2[:], in1=msq[:], op=ALU.subtract)
-        nc.scalar.activation(out=vt3[:, :, JT : 2 * JT], in_=v3(var[:], JT), func=ACT.Sqrt)
-        nc.vector.tensor_reduce(out=st[:, 4:8], in_=v3(t2[:], JT), axis=AX.X, op=ALU.add)
-        nc.vector.tensor_reduce(out=st[:, 0:4], in_=vt3, axis=AX.X, op=ALU.add)
-        tot = psm.tile([P, 8], F32, name="tot", tag="misc")
-        nc.tensor.matmul(out=tot[:], lhsT=ones[:], rhs=st[:], start=True, stop=True)
-        nc.vector.tensor_scalar(out=mom[:], in0=tot[:], scalar1=1.0 / (2 * C), scalar2=None, op0=ALU.mult)
-        nc.vector.tensor_tensor(out=musq[:], in0=mom[:, 0:4], in1=mom[:, 0:4], op=ALU.mult)
-        nc.vector.scalar_tensor_tensor(
-            out=vle[:], in0=mom[:, 4:8], scalar=EPS_LN, in1=musq[:], op0=ALU.add, op1=ALU.subtract
-        )
-        nc.scalar.activation(out=sd[:], in_=vle[:], func=ACT.Sqrt)
-        nc.vector.reciprocal(out=rstd[:], in_=sd[:])
+        nc.scalar.activation(out=vt3[:, :, JT : 2 * JT], in_=v3(var[:]), func=ACT.Sqrt)
+        nc.vector.tensor_reduce(out=st3[:, 1, :], in_=v3(t2[:]), axis=AX.X, op=ALU.add)
+        nc.vector.tensor_reduce(out=st3[:, 0, :], in_=vt3, axis=AX.X, op=ALU.add)
+        fin = psm.tile([P, 512], F32, name="fin", tag="misc")
+        nc.tensor.transpose(fin[:, 0:P], vt[:], ident[:])
         for b in range(B):
-            nc.vector.tensor_scalar(
-                out=vn[:, b * 24 : (b + 1) * 24], in0=vt[:, b * 24 : (b + 1) * 24],
-                scalar1=mom[:, b : b + 1], scalar2=rstd[:, b : b + 1], op0=ALU.subtract, op1=ALU.mult,
+            nc.tensor.matmul(
+                out=fin[:, P : P + 2], lhsT=sel[:, b, :], rhs=st[:, 2 * b : 2 * b + 2],
+                start=(b == 0), stop=(b == B - 1),
             )
-        vnt = psm.tile([P, P], F32, name="vnt", tag="misc")
-        nc.tensor.transpose(vnt[:], vn[:], ident[:])
-        nc.vector.tensor_tensor(out=o1[0:96, :], in0=vnt[0:96, :], in1=g2t[0:96, :], op=ALU.mult)
-        nc.vector.tensor_tensor(out=o2[0:96, :], in0=o1[0:96, :], in1=be2t[0:96, :], op=ALU.add)
-        nc.sync.dma_start(out=out.rearrange("b (j p) o -> (b j) (p o)", p=P), in_=o2[0:96, :])
+        nc.vector.tensor_scalar(out=mom[:], in0=fin[:, P : P + 2], scalar1=1.0 / (2 * C), scalar2=None, op0=ALU.mult)
+        nc.vector.scalar_tensor_tensor(
+            out=nv[:], in0=mom[:, 0:1], scalar=mom[:, 0:1], in1=mom[:, 1:2], op0=ALU.mult, op1=ALU.subtract
+        )
+        nc.scalar.activation(out=sd[:], in_=nv[:], func=ACT.Sqrt, bias=epst[:, 0:1], scale=-1.0)
+        nc.vector.scalar_tensor_tensor(
+            out=o1[0:R, :], in0=fin[0:R, 0:P], scalar=mom[0:R, 0:1], in1=g2t[0:R, :], op0=ALU.subtract, op1=ALU.mult
+        )
+        nc.vector.reciprocal(out=rstd[:], in_=sd[:])
+        nc.vector.scalar_tensor_tensor(
+            out=o2[0:R, :], in0=o1[0:R, :], scalar=rstd[0:R, 0:1], in1=be2t[0:R, :], op0=ALU.mult, op1=ALU.add
+        )
+        nc.sync.dma_start(out=out.rearrange("b (j p) o -> (b j) (p o)", p=P), in_=o2[0:R, :])

@@ -36,7 +36,7 @@ def tile_attentivestatspool_pb_kernel(tc, h, x, mask, w2_words, w2_scales, b2, g
         namp = ctx.enter_context(tc.tile_pool(name="namp", bufs=3))
         ep = ctx.enter_context(tc.tile_pool(name="ep", bufs=7))
         pp = ctx.enter_context(tc.tile_pool(name="pp", bufs=3))
-        gp = ctx.enter_context(tc.tile_pool(name="gp", bufs=1))
+        gp = ctx.enter_context(tc.tile_pool(name="gp", bufs=2))
         psa = ctx.enter_context(tc.psum_pool(name="psa", bufs=3))
         psb = ctx.enter_context(tc.psum_pool(name="psb", bufs=4))
         psm = ctx.enter_context(tc.psum_pool(name="psm", bufs=1))
@@ -62,6 +62,7 @@ def tile_attentivestatspool_pb_kernel(tc, h, x, mask, w2_words, w2_scales, b2, g
         pbrow = const.tile([P, P], F32, name="pbrow")
         pb = const.tile([P, 16], F32, name="pb")
         ident = const.tile([P, P], F32, name="ident")
+        identb = const.tile([P, P], BF16, name="identb")
         sel = const.tile([P, B, P], F32, name="sel")
         warm = const.tile([P, 1], F32, name="warm")
         warm2 = const.tile([P, 1], F32, name="warm2")
@@ -95,19 +96,20 @@ def tile_attentivestatspool_pb_kernel(tc, h, x, mask, w2_words, w2_scales, b2, g
             )
         nc.sync.dma_start(out=wwords[:].bitcast(I32), in_=w2_words[0].bitcast(I32))
         load_h(1)
-        for cb in range(NCB):
-            load_x(cb)
-        for b in range(1, B):
-            if b + 1 < B:
-                load_h(b + 1)
-            for cb in range(NCB):
-                load_x(b * NCB + cb)
+        load_x(0)
+        load_h(2)
+        load_x(1)
+        load_x(2)
+        load_h(3)
+        for g in range(NCB, NG):
+            load_x(g)
         for b in range(B):
             nc.sync.dma_start(out=g2t[b * 24 : (b + 1) * 24, :], in_=g2.rearrange("(j p) -> j p", p=P))
             nc.sync.dma_start(out=be2t[b * 24 : (b + 1) * 24, :], in_=be2.rearrange("(j p) -> j p", p=P))
 
         nc.gpsimd.memset(warm[:], 1.0)
         make_identity(nc, ident[:])
+        make_identity(nc, identb[:])
         nc.scalar.activation(out=warm2[:], in_=warm[:], func=ACT.Exp)
         nc.gpsimd.memset(vt[:], 0.0)
         nc.gpsimd.memset(epst[:], EPS_LN)
@@ -131,8 +133,10 @@ def tile_attentivestatspool_pb_kernel(tc, h, x, mask, w2_words, w2_scales, b2, g
             src = hraw[b][:, :, k * P : (k + 1) * P].rearrange("p j t -> p t j")
             if eng == "v":
                 nc.vector.tensor_copy(out=dst, in_=src)
-            else:
+            elif eng == "s":
                 nc.scalar.copy(out=dst, in_=src)
+            else:
+                nc.gpsimd.tensor_scalar(out=dst, in0=src, scalar1=1.0, scalar2=0.0, op0=ALU.mult, op1=ALU.add)
 
         def quantize(b, lo, hi):
             nc.vector.quantize_mx(
@@ -186,7 +190,7 @@ def tile_attentivestatspool_pb_kernel(tc, h, x, mask, w2_words, w2_scales, b2, g
                 nt = namp.tile([P, 4, 512], F32, name="nam")
                 nam[g] = nt
             col = b * 4 + tb
-            if j in (1, 3):
+            if j in (1, 3, 5):
                 nc.vector.tensor_scalar(
                     out=nam[g][:, tb, :], in0=pa[j][:], scalar1=-1.0, scalar2=pb[:, col : col + 1],
                     op0=ALU.mult, op1=ALU.add,
@@ -226,80 +230,156 @@ def tile_attentivestatspool_pb_kernel(tc, h, x, mask, w2_words, w2_scales, b2, g
             g, cc = divmod(i, 4)
             return xs[g][:, cc, :]
 
+        xpt = {}
+        pgt = {}
+
+        def xp(i):
+            if not 0 <= i < NT:
+                return
+            xq = psm.tile([P, 512], F32, name="xq", tag="misc")
+            xpt[i] = xq
+            nc.tensor.matmul(out=xq[:], lhsT=identb[:], rhs=xtile(i), start=True, stop=True)
+
+        def xin(i):
+            if i in xpt:
+                return xpt[i][:]
+            return xtile(i)
+
         def prod1(i):
             p1 = pp.tile([P, 512], F32, name="p1")
             pt[i] = p1
             nc.vector.scalar_tensor_tensor(
-                out=p1[:], in0=et[i][:], scalar=1.0, in1=xtile(i), op0=ALU.mult, op1=ALU.mult,
+                out=p1[:], in0=et[i][:], scalar=1.0, in1=xin(i), op0=ALU.mult, op1=ALU.mult,
                 accum_out=s1[:, i : i + 1],
             )
 
-        def prod1_gpsimd(i):
+        def new_pg(i):
             pg = gp.tile([P, 512], F32, name="pg")
+            pgt[i] = pg
             pt[i] = pg
-            nc.gpsimd.tensor_tensor(out=pg[:], in0=et[i][:], in1=xtile(i), op=ALU.mult)
+
+        def prod1_gpsimd(i):
+            nc.gpsimd.tensor_tensor(out=pt[i][:], in0=et[i][:], in1=xtile(i), op=ALU.mult)
 
         def sum1_scalar(i):
             sj = gp.tile([P, 512], BF16, name="sj")
             nc.scalar.activation(out=sj[:], in_=pt[i][:], func=ACT.Identity, accum_out=s1[:, i : i + 1])
 
-        def prod2(i):
-            p2 = pp.tile([P, 512], F32, name="p2")
+        def prod2(i, junk):
             nc.vector.scalar_tensor_tensor(
-                out=p2[:], in0=pt[i][:], scalar=1.0, in1=xtile(i), op0=ALU.mult, op1=ALU.mult,
+                out=junk[:], in0=pt[i][:], scalar=1.0, in1=xin(i), op0=ALU.mult, op1=ALU.mult,
                 accum_out=s2[:, i : i + 1],
             )
 
-        for v in range(-4, NR):
-            a = 3 * v
-            na = a + 3
-            ta = a + 6
-            j0 = a + 9
-            helped = 0 <= v < NR - 1
-            ev(j0)
-            ev(j0 + 1)
-            mn(na)
-            mn(na + 1)
-            mn(na + 2)
-            if helped:
-                prod1_gpsimd(a)
-            ex(na)
-            ev(j0 + 2)
-            tr(ta)
-            tr(ta + 1)
-            ex(na + 1)
-            tr(ta + 2)
-            if helped:
-                sum1_scalar(a)
-            ex(na + 2)
-            for b in range(2, B):
-                k = v - (4 * b - 8)
-                if 0 <= k < 4:
-                    if k == 0:
-                        new_hil(b)
-                    interleave(b, k, "s")
-            if v >= 0:
-                if not helped:
-                    prod1(a)
-                prod1(a + 1)
-                prod1(a + 2)
-                prod2(a + 1)
-                prod2(a + 2)
-                for b in range(1, B):
-                    if v == 4 * b - 4:
-                        quantize(b, 0, T)
-                prod2(a)
-            mx(j0 + 3)
-            mx(j0 + 4)
-            mx(j0 + 5)
+        def new_junk():
+            p2 = pp.tile([P, 512], F32, name="p2")
+            return p2
 
         def v3(ap):
             return ap.rearrange("p (b j) -> p b j", b=B)
 
         vt3 = v3(vt[:, 0 : 2 * NT])
         r0 = const.tile([P, NT], F32, name="r0")
-        ex2 = const.tile([P, NT], F32, name="ex2")
         msq = const.tile([P, NT], F32, name="msq")
+
+        mx(0)
+        mx(1)
+        mx(2)
+        ev(0)
+        ev(1)
+        mx(3)
+        mx(4)
+        ev(2)
+        mx(5)
+        ev(3)
+        ev(4)
+        ev(5)
+        tr(0)
+        tr(1)
+        mx(6)
+        mx(7)
+        tr(2)
+        tr(3)
+        mx(8)
+        xp(1)
+        mn(0)
+        ex(0)
+        mn(1)
+        ex(1)
+        ev(6)
+        ev(7)
+        mn(2)
+        ex(2)
+        ev(8)
+        tr(4)
+        tr(5)
+        mx(9)
+        mx(10)
+        mx(11)
+
+        for v in range(NR):
+            a = 3 * v
+            na = a + 3
+            ta = a + 6
+            j0 = a + 9
+            helped = v < NR - 1
+            last = v == NR - 1
+            ev(j0)
+            mn(na)
+            if v == 0:
+                quantize(1, 0, T)
+            if helped:
+                if a not in pgt:
+                    new_pg(a)
+                prod1_gpsimd(a)
+            else:
+                prod1(a)
+            for b in range(2, B):
+                k = v - (4 * b - 8)
+                if 0 <= k < 4:
+                    if k == 0:
+                        new_hil(b)
+                    interleave(b, k, "g")
+            prod1(a + 1)
+            if last:
+                nc.vector.reciprocal(out=r0[:], in_=s0[:])
+            ex(na)
+            tr(ta)
+            ev(j0 + 1)
+            mn(na + 1)
+            tr(ta + 1)
+            mx(j0 + 3)
+            mx(j0 + 4)
+            if last:
+                prod1(a + 2)
+                prod2(a, new_junk())
+                nc.vector.tensor_tensor(out=vt3[:, :, 0:JT], in0=v3(s1[:]), in1=v3(r0[:]), op=ALU.mult)
+            prod2(a + 1, new_junk())
+            xp(a + 4)
+            ex(na + 1)
+            if helped:
+                sum1_scalar(a)
+            mn(na + 2)
+            ex(na + 2)
+            ev(j0 + 2)
+            tr(ta + 2)
+            mx(j0 + 5)
+            if last:
+                nc.vector.tensor_tensor(out=v3(msq[:]), in0=vt3[:, :, 0:JT], in1=vt3[:, :, 0:JT], op=ALU.mult)
+                prod2(a + 2, new_junk())
+            else:
+                prod1(a + 2)
+                prod2(a, new_junk())
+                for b in range(2, B):
+                    if v == 4 * b - 5:
+                        quantize(b, 0, T)
+                if v + 1 < NR - 1:
+                    new_pg(a + 3)
+                    prod2(a + 2, pgt[a + 3])
+                else:
+                    prod2(a + 2, new_junk())
+
+        ex2 = const.tile([P, NT], F32, name="ex2")
         t2 = const.tile([P, NT], F32, name="t2")
         var = const.tile([P, NT], F32, name="var")
         st = const.tile([P, 2 * B], F32, name="st")
@@ -312,10 +392,7 @@ def tile_attentivestatspool_pb_kernel(tc, h, x, mask, w2_words, w2_scales, b2, g
         st3 = st[:].rearrange("p (b k) -> p k b", k=2)
         R = 2 * JT * B
 
-        nc.vector.reciprocal(out=r0[:], in_=s0[:])
-        nc.vector.tensor_tensor(out=vt3[:, :, 0:JT], in0=v3(s1[:]), in1=v3(r0[:]), op=ALU.mult)
         nc.vector.tensor_tensor(out=ex2[:], in0=s2[:], in1=r0[:], op=ALU.mult)
-        nc.vector.tensor_tensor(out=v3(msq[:]), in0=vt3[:, :, 0:JT], in1=vt3[:, :, 0:JT], op=ALU.mult)
         nc.vector.scalar_tensor_tensor(
             out=t2[:], in0=msq[:], scalar=EPS_STD, in1=ex2[:], op0=ALU.add, op1=ALU.max
         )
@@ -342,4 +419,6 @@ def tile_attentivestatspool_pb_kernel(tc, h, x, mask, w2_words, w2_scales, b2, g
         nc.vector.scalar_tensor_tensor(
             out=o2[0:R, :], in0=o1[0:R, :], scalar=rstd[0:R, 0:1], in1=be2t[0:R, :], op0=ALU.mult, op1=ALU.add
         )
-        nc.sync.dma_start(out=out.rearrange("b (j p) o -> (b j) (p o)", p=P), in_=o2[0:R, :])
+        outr = out.rearrange("b (j p) o -> (b j) (p o)", p=P)
+        nc.sync.dma_start(out=outr[0:64, :], in_=o2[0:64, :])
+        nc.scalar.dma_start(out=outr[64:R, :], in_=o2[64:R, :])

@@ -63,7 +63,9 @@ def tile_attentivestatspool_pb_kernel(tc, h, x, mask, w2_words, w2_scales, b2, g
         pb = const.tile([P, 16], F32, name="pb")
         ident = const.tile([P, P], F32, name="ident")
         identb = const.tile([P, P], BF16, name="identb")
-        sel = const.tile([P, B, P], F32, name="sel")
+        ones = const.tile([P, P], F32, name="ones")
+        ysel = const.tile([P, P], F32, name="ysel")
+        oh = const.tile([P, B], F32, name="oh")
         warm = const.tile([P, 1], F32, name="warm")
         warm2 = const.tile([P, 1], F32, name="warm2")
         epst = const.tile([P, 1], F32, name="epst")
@@ -89,6 +91,12 @@ def tile_attentivestatspool_pb_kernel(tc, h, x, mask, w2_words, w2_scales, b2, g
         nc.gpsimd.memset(mrow[:], 0.0)
         nc.scalar.dma_start(out=mrow[0:16, :], in_=mask.rearrange("b o (tb p) -> (b o tb) p", p=P))
         nc.vector.memset(wplane[:].bitcast(I32), 0)
+        nc.vector.memset(ysel[:], 0.0)
+        for b in range(B):
+            nc.vector.memset(ysel[32 * b : 32 * (b + 1), 24 * b : 24 * (b + 1)], 1.0)
+        nc.vector.memset(ones[:], 1.0)
+        nc.vector.memset(vt[:], 0.0)
+        nc.vector.memset(epst[:], EPS_LN)
         for q in range(4):
             nc.sync.dma_start(
                 out=wplane[32 * q : 32 * q + 4, :].bitcast(I32),
@@ -107,18 +115,15 @@ def tile_attentivestatspool_pb_kernel(tc, h, x, mask, w2_words, w2_scales, b2, g
             nc.sync.dma_start(out=g2t[b * 24 : (b + 1) * 24, :], in_=g2.rearrange("(j p) -> j p", p=P))
             nc.sync.dma_start(out=be2t[b * 24 : (b + 1) * 24, :], in_=be2.rearrange("(j p) -> j p", p=P))
 
-        nc.gpsimd.memset(warm[:], 1.0)
         make_identity(nc, ident[:])
+        nc.gpsimd.memset(warm[:], 1.0)
         make_identity(nc, identb[:])
         nc.scalar.activation(out=warm2[:], in_=warm[:], func=ACT.Exp)
-        nc.gpsimd.memset(vt[:], 0.0)
-        nc.gpsimd.memset(epst[:], EPS_LN)
-        nc.gpsimd.memset(sel[:], 0.0)
-        for b in range(B):
-            nc.gpsimd.memset(sel[:, b, 24 * b : 24 * (b + 1)], 1.0)
 
-        nc.gpsimd.tensor_scalar(out=pbrow[:], in0=mrow[:], scalar1=-BIG, scalar2=BIG, op0=ALU.mult, op1=ALU.add)
         pbt = psm.tile([P, 512], F32, name="pbt", tag="misc")
+        nc.tensor.transpose(pbt[:, P : 2 * P], ysel[:], ident[:])
+        nc.vector.tensor_copy(out=oh[:], in_=pbt[:, P : 2 * P : 32])
+        nc.vector.tensor_scalar(out=pbrow[:], in0=mrow[:], scalar1=-BIG, scalar2=BIG, op0=ALU.mult, op1=ALU.add)
         nc.tensor.transpose(pbt[:, 0:P], pbrow[:], ident[:])
         nc.scalar.copy(out=pb[:], in_=pbt[:, 0:16])
 
@@ -258,6 +263,10 @@ def tile_attentivestatspool_pb_kernel(tc, h, x, mask, w2_words, w2_scales, b2, g
             pgt[i] = pg
             pt[i] = pg
 
+        def new_pg2(i):
+            pg2 = gp.tile([P, 512], F32, name="pg2")
+            pt[i] = pg2
+
         def prod1_gpsimd(i):
             nc.gpsimd.tensor_tensor(out=pt[i][:], in0=et[i][:], in1=xtile(i), op=ALU.mult)
 
@@ -323,6 +332,7 @@ def tile_attentivestatspool_pb_kernel(tc, h, x, mask, w2_words, w2_scales, b2, g
             ta = a + 6
             j0 = a + 9
             helped = v < NR - 1
+            two = helped and v % 2 == 0
             last = v == NR - 1
             ev(j0)
             mn(na)
@@ -334,12 +344,17 @@ def tile_attentivestatspool_pb_kernel(tc, h, x, mask, w2_words, w2_scales, b2, g
                 prod1_gpsimd(a)
             else:
                 prod1(a)
+            if two:
+                new_pg2(a + 2)
+                prod1_gpsimd(a + 2)
             for b in range(2, B):
-                k = v - (4 * b - 8)
-                if 0 <= k < 4:
-                    if k == 0:
-                        new_hil(b)
-                    interleave(b, k, "g")
+                if v == 4 * b - 7:
+                    new_hil(b)
+                    interleave(b, 0, "g")
+                    interleave(b, 1, "g")
+                if v == 4 * b - 5:
+                    interleave(b, 2, "g")
+                    interleave(b, 3, "g")
             prod1(a + 1)
             if last:
                 nc.vector.reciprocal(out=r0[:], in_=s0[:])
@@ -361,6 +376,8 @@ def tile_attentivestatspool_pb_kernel(tc, h, x, mask, w2_words, w2_scales, b2, g
                 sum1_scalar(a)
             mn(na + 2)
             ex(na + 2)
+            if two:
+                sum1_scalar(a + 2)
             ev(j0 + 2)
             tr(ta + 2)
             mx(j0 + 5)
@@ -368,7 +385,8 @@ def tile_attentivestatspool_pb_kernel(tc, h, x, mask, w2_words, w2_scales, b2, g
                 nc.vector.tensor_tensor(out=v3(msq[:]), in0=vt3[:, :, 0:JT], in1=vt3[:, :, 0:JT], op=ALU.mult)
                 prod2(a + 2, new_junk())
             else:
-                prod1(a + 2)
+                if not two:
+                    prod1(a + 2)
                 prod2(a, new_junk())
                 for b in range(2, B):
                     if v == 4 * b - 5:
@@ -389,7 +407,7 @@ def tile_attentivestatspool_pb_kernel(tc, h, x, mask, w2_words, w2_scales, b2, g
         rstd = const.tile([P, 1], F32, name="rstd")
         o1 = const.tile([P, P], F32, name="o1")
         o2 = const.tile([P, P], F32, name="o2")
-        st3 = st[:].rearrange("p (b k) -> p k b", k=2)
+        mj = const.tile([P, 2 * B], F32, name="mj")
         R = 2 * JT * B
 
         nc.vector.tensor_tensor(out=ex2[:], in0=s2[:], in1=r0[:], op=ALU.mult)
@@ -398,16 +416,16 @@ def tile_attentivestatspool_pb_kernel(tc, h, x, mask, w2_words, w2_scales, b2, g
         )
         nc.vector.tensor_tensor(out=var[:], in0=t2[:], in1=msq[:], op=ALU.subtract)
         nc.scalar.activation(out=vt3[:, :, JT : 2 * JT], in_=v3(var[:]), func=ACT.Sqrt)
-        nc.vector.tensor_reduce(out=st3[:, 1, :], in_=v3(t2[:]), axis=AX.X, op=ALU.add)
-        nc.vector.tensor_reduce(out=st3[:, 0, :], in_=vt3, axis=AX.X, op=ALU.add)
+        nc.vector.tensor_reduce(out=st[:, B : 2 * B], in_=v3(t2[:]), axis=AX.X, op=ALU.add)
+        nc.vector.tensor_reduce(out=st[:, 0:B], in_=vt3, axis=AX.X, op=ALU.add)
         fin = psm.tile([P, 512], F32, name="fin", tag="misc")
         nc.tensor.transpose(fin[:, 0:P], vt[:], ident[:])
-        for b in range(B):
-            nc.tensor.matmul(
-                out=fin[:, P : P + 2], lhsT=sel[:, b, :], rhs=st[:, 2 * b : 2 * b + 2],
-                start=(b == 0), stop=(b == B - 1),
+        nc.tensor.matmul(out=fin[:, P : P + 2 * B], lhsT=ones[:], rhs=st[:], start=True, stop=True)
+        for k in range(2):
+            nc.vector.scalar_tensor_tensor(
+                out=mj[:, k * B : (k + 1) * B], in0=fin[:, P + k * B : P + (k + 1) * B], scalar=1.0 / (2 * C),
+                in1=oh[:], op0=ALU.mult, op1=ALU.mult, accum_out=mom[:, k : k + 1],
             )
-        nc.vector.tensor_scalar(out=mom[:], in0=fin[:, P : P + 2], scalar1=1.0 / (2 * C), scalar2=None, op0=ALU.mult)
         nc.vector.scalar_tensor_tensor(
             out=nv[:], in0=mom[:, 0:1], scalar=mom[:, 0:1], in1=mom[:, 1:2], op0=ALU.mult, op1=ALU.subtract
         )

@@ -38,7 +38,9 @@ def tile_attentivestatspool_pb_kernel(tc, h, x, mask, w2_words, w2_scales, b2, g
         pp = ctx.enter_context(tc.tile_pool(name="pp", bufs=3))
         gp = ctx.enter_context(tc.tile_pool(name="gp", bufs=2))
         psa = ctx.enter_context(tc.psum_pool(name="psa", bufs=3))
-        psb = ctx.enter_context(tc.psum_pool(name="psb", bufs=4))
+        psb = ctx.enter_context(tc.psum_pool(name="psb", bufs=3))
+        psf = ctx.enter_context(tc.psum_pool(name="psf", bufs=1))
+        fp = ctx.enter_context(tc.tile_pool(name="fp", bufs=2))
         psm = ctx.enter_context(tc.psum_pool(name="psm", bufs=1))
         ctx.enter_context(tc.manual_schedule())
 
@@ -162,6 +164,9 @@ def tile_attentivestatspool_pb_kernel(tc, h, x, mask, w2_words, w2_scales, b2, g
             out=hil[1][:], in0=hraw[1][:].rearrange("p j t -> p t j"), scalar1=1.0, scalar2=0.0,
             op0=ALU.mult, op1=ALU.add,
         )
+        new_hil(2)
+        interleave(2, 0, "g")
+        interleave(2, 1, "g")
 
         pa = {}
         nam = {}
@@ -274,6 +279,27 @@ def tile_attentivestatspool_pb_kernel(tc, h, x, mask, w2_words, w2_scales, b2, g
             sj = gp.tile([P, 512], BF16, name="sj")
             nc.scalar.activation(out=sj[:], in_=pt[i][:], func=ACT.Identity, accum_out=s1[:, i : i + 1])
 
+        fs = psf.tile([P, 512], F32, name="fs")
+        fsb = {}
+
+        def fold(i, region):
+            for tb in range(4):
+                nc.tensor.matmul(
+                    out=fs[:, region * P : (region + 1) * P], lhsT=pt[i][:, tb * P : (tb + 1) * P], rhs=ident[:],
+                    is_transpose=True, start=(tb == 0), stop=(tb == 3),
+                )
+
+        def fold_out(v, regions):
+            fb = fp.tile([P, 3 * P], F32, name="fb")
+            fsb[v] = fb
+            nc.scalar.copy(out=fb[:, 0 : regions * P], in_=fs[:, 0 : regions * P])
+
+        def fold_sum(v, region, col):
+            nc.tensor.matmul(
+                out=fs[:, 3 * P + col : 3 * P + col + 1], lhsT=fsb[v][:, region * P : (region + 1) * P],
+                rhs=ones[:, 0:1], start=True, stop=True,
+            )
+
         def prod2(i, junk):
             nc.vector.scalar_tensor_tensor(
                 out=junk[:], in0=pt[i][:], scalar=1.0, in1=xin(i), op0=ALU.mult, op1=ALU.mult,
@@ -308,11 +334,11 @@ def tile_attentivestatspool_pb_kernel(tc, h, x, mask, w2_words, w2_scales, b2, g
         mx(6)
         mx(7)
         tr(2)
-        tr(3)
         mx(8)
         xp(1)
         mn(0)
         ex(0)
+        tr(3)
         mn(1)
         ex(1)
         ev(6)
@@ -332,8 +358,10 @@ def tile_attentivestatspool_pb_kernel(tc, h, x, mask, w2_words, w2_scales, b2, g
             ta = a + 6
             j0 = a + 9
             helped = v < NR - 1
-            two = helped and v % 2 == 0
+            two = helped
             last = v == NR - 1
+            by_pe = v < NR - 2
+            pe_before = 1 <= v < NR - 1
             ev(j0)
             mn(na)
             if v == 0:
@@ -347,22 +375,15 @@ def tile_attentivestatspool_pb_kernel(tc, h, x, mask, w2_words, w2_scales, b2, g
             if two:
                 new_pg2(a + 2)
                 prod1_gpsimd(a + 2)
-            for b in range(2, B):
-                if v == 4 * b - 7:
-                    new_hil(b)
-                    interleave(b, 0, "g")
-                    interleave(b, 1, "g")
-                if v == 4 * b - 5:
-                    interleave(b, 2, "g")
-                    interleave(b, 3, "g")
             prod1(a + 1)
             if last:
                 nc.vector.reciprocal(out=r0[:], in_=s0[:])
+                npe = NR - 2
+                nc.vector.tensor_copy(out=s1[:, 0 : 3 * npe : 3], in_=fs[:, 3 * P : 3 * P + npe])
             ex(na)
             tr(ta)
             ev(j0 + 1)
             mn(na + 1)
-            tr(ta + 1)
             mx(j0 + 3)
             mx(j0 + 4)
             if last:
@@ -372,15 +393,27 @@ def tile_attentivestatspool_pb_kernel(tc, h, x, mask, w2_words, w2_scales, b2, g
             prod2(a + 1, new_junk())
             xp(a + 4)
             ex(na + 1)
-            if helped:
+            tr(ta + 1)
+            if helped and not by_pe:
                 sum1_scalar(a)
+            if pe_before:
+                fold_out(v - 1, 1)
             mn(na + 2)
             ex(na + 2)
             if two:
                 sum1_scalar(a + 2)
             ev(j0 + 2)
+            if v < 6:
+                b, k = (2, 2 + v) if v < 2 else (3, v - 2)
+                if k == 0:
+                    new_hil(b)
+                interleave(b, k, "s")
             tr(ta + 2)
             mx(j0 + 5)
+            if pe_before:
+                fold_sum(v - 1, 0, v - 1)
+            if by_pe:
+                fold(a, 0)
             if last:
                 nc.vector.tensor_tensor(out=v3(msq[:]), in0=vt3[:, :, 0:JT], in1=vt3[:, :, 0:JT], op=ALU.mult)
                 prod2(a + 2, new_junk())

@@ -300,6 +300,20 @@ def tile_attentivestatspool_pb_kernel(tc, h, x, mask, w2_words, w2_scales, b2, g
                 rhs=ones[:, 0:1], start=True, stop=True,
             )
 
+        def xp_spare(i):
+            xq = psa.tile([P, 512], F32, name="psA")
+            xpt[i] = xq
+            nc.tensor.matmul(out=xq[:], lhsT=identb[:], rhs=xtile(i), start=True, stop=True)
+
+        def prod2_gpsimd(i):
+            pq = gp.tile([P, 512], F32, name="pq")
+            nc.gpsimd.tensor_tensor(out=pq[:], in0=pt[i][:], in1=xtile(i), op=ALU.mult)
+            return pq
+
+        def sum2_scalar(i, pq):
+            sj = gp.tile([P, 512], BF16, name="sj")
+            nc.scalar.activation(out=sj[:], in_=pq[:], func=ACT.Identity, accum_out=s2[:, i : i + 1])
+
         def prod2(i, junk):
             nc.vector.scalar_tensor_tensor(
                 out=junk[:], in0=pt[i][:], scalar=1.0, in1=xin(i), op0=ALU.mult, op1=ALU.mult,
@@ -366,12 +380,12 @@ def tile_attentivestatspool_pb_kernel(tc, h, x, mask, w2_words, w2_scales, b2, g
             mn(na)
             if v == 0:
                 quantize(1, 0, T)
-            if helped:
-                if a not in pgt:
-                    new_pg(a)
-                prod1_gpsimd(a)
-            else:
-                prod1(a)
+            if a not in pgt:
+                new_pg(a)
+            prod1_gpsimd(a)
+            if last:
+                xp_spare(a + 2)
+                pq_last = prod2_gpsimd(a)
             if two:
                 new_pg2(a + 2)
                 prod1_gpsimd(a + 2)
@@ -388,14 +402,14 @@ def tile_attentivestatspool_pb_kernel(tc, h, x, mask, w2_words, w2_scales, b2, g
             mx(j0 + 4)
             if last:
                 prod1(a + 2)
-                prod2(a, new_junk())
-                nc.vector.tensor_tensor(out=vt3[:, :, 0:JT], in0=v3(s1[:]), in1=v3(r0[:]), op=ALU.mult)
             prod2(a + 1, new_junk())
             xp(a + 4)
             ex(na + 1)
             tr(ta + 1)
-            if helped and not by_pe:
+            if not by_pe:
                 sum1_scalar(a)
+            if last:
+                sum2_scalar(a, pq_last)
             if pe_before:
                 fold_out(v - 1, 1)
             mn(na + 2)
@@ -415,8 +429,9 @@ def tile_attentivestatspool_pb_kernel(tc, h, x, mask, w2_words, w2_scales, b2, g
             if by_pe:
                 fold(a, 0)
             if last:
-                nc.vector.tensor_tensor(out=v3(msq[:]), in0=vt3[:, :, 0:JT], in1=vt3[:, :, 0:JT], op=ALU.mult)
                 prod2(a + 2, new_junk())
+                nc.vector.tensor_tensor(out=vt3[:, :, 0:JT], in0=v3(s1[:]), in1=v3(r0[:]), op=ALU.mult)
+                nc.vector.tensor_tensor(out=v3(msq[:]), in0=vt3[:, :, 0:JT], in1=vt3[:, :, 0:JT], op=ALU.mult)
             else:
                 if not two:
                     prod1(a + 2)
@@ -424,7 +439,7 @@ def tile_attentivestatspool_pb_kernel(tc, h, x, mask, w2_words, w2_scales, b2, g
                 for b in range(2, B):
                     if v == 4 * b - 5:
                         quantize(b, 0, T)
-                if v + 1 < NR - 1:
+                if v + 1 < NR:
                     new_pg(a + 3)
                     prod2(a + 2, pgt[a + 3])
                 else:

@@ -394,6 +394,7 @@ def tile_attentivestatspool_pb_kernel(tc, h, x, mask, w2_words, w2_scales, b2, g
                 nc.vector.reciprocal(out=r0[:], in_=s0[:])
                 npe = NR - 2
                 nc.vector.tensor_copy(out=s1[:, 0 : 3 * npe : 3], in_=fs[:, 3 * P : 3 * P + npe])
+                nc.vector.tensor_copy(out=s1[:, 2 : 3 * npe : 3], in_=fs[:, 3 * P + 16 : 3 * P + 16 + npe])
             ex(na)
             tr(ta)
             ev(j0 + 1)
@@ -411,10 +412,10 @@ def tile_attentivestatspool_pb_kernel(tc, h, x, mask, w2_words, w2_scales, b2, g
             if last:
                 sum2_scalar(a, pq_last)
             if pe_before:
-                fold_out(v - 1, 1)
+                fold_out(v - 1, 2)
             mn(na + 2)
             ex(na + 2)
-            if two:
+            if two and not by_pe:
                 sum1_scalar(a + 2)
             ev(j0 + 2)
             if v < 6:
@@ -426,8 +427,10 @@ def tile_attentivestatspool_pb_kernel(tc, h, x, mask, w2_words, w2_scales, b2, g
             mx(j0 + 5)
             if pe_before:
                 fold_sum(v - 1, 0, v - 1)
+                fold_sum(v - 1, 1, 16 + v - 1)
             if by_pe:
                 fold(a, 0)
+                fold(a + 2, 1)
             if last:
                 prod2(a + 2, new_junk())
                 nc.vector.tensor_tensor(out=vt3[:, :, 0:JT], in0=v3(s1[:]), in1=v3(r0[:]), op=ALU.mult)

@@ -438,15 +438,12 @@ def tile_attentivestatspool_pb_kernel(tc, h, x, mask, w2_words, w2_scales, b2, g
             else:
                 if not two:
                     prod1(a + 2)
-                prod2(a, new_junk())
                 for b in range(2, B):
                     if v == 4 * b - 5:
                         quantize(b, 0, T)
-                if v + 1 < NR:
-                    new_pg(a + 3)
-                    prod2(a + 2, pgt[a + 3])
-                else:
-                    prod2(a + 2, new_junk())
+                new_pg(a + 3)
+                prod2(a, pgt[a + 3])
+                prod2(a + 2, new_junk())
 
         ex2 = const.tile([P, NT], F32, name="ex2")
         t2 = const.tile([P, NT], F32, name="t2")

@@ -138,6 +138,9 @@ def tile_attentivestatspool_pb_kernel(tc, h, x, mask, w2_words, w2_scales, b2, g
         def interleave(b, k, eng):
             dst = hil[b][:, k * P : (k + 1) * P, :]
             src = hraw[b][:, :, k * P : (k + 1) * P].rearrange("p j t -> p t j")
+            if eng != "g":
+                dst = hil[b][:, k * P : (k + 1) * P, :].rearrange("p (c i) j -> p c j i", i=4)
+                src = hraw[b][:, :, k * P : (k + 1) * P].rearrange("p j (c i) -> p c j i", i=4)
             if eng == "v":
                 nc.vector.tensor_copy(out=dst, in_=src)
             elif eng == "s":

@@ -177,22 +177,24 @@ def tile_attentivestatspool_pb_kernel(tc, h, x, mask, w2_words, w2_scales, b2, g
         et = {}
         pt = {}
 
-        def mx(j):
-            if not 0 <= j < NT:
+        def mx(j, times=1):
+            if j < 0:
                 return
-            g, tb = divmod(j, 4)
+            g, tb = divmod(min(j, NT - 1), 4)
             b, cb = divmod(g, NCB)
             a = psa.tile([P, 512], F32, name="psA")
-            pa[j] = a
-            nc.tensor.matmul_mx(
-                out=a[:],
-                lhsT=codes[b][:, tb * P : (tb + 1) * P].bitcast(E5M2X4),
-                lhsT_scale=hsc[b][:, tb * P : (tb + 1) * P],
-                rhs=wwords[:, cb * 1024 : (cb + 1) * 1024].bitcast(E2M1X4),
-                rhs_scale=wplane[:, cb * 512 : (cb + 1) * 512],
-                start=True,
-                stop=True,
-            )
+            if j < NT:
+                pa[j] = a
+            for rpt in range(times):
+                nc.tensor.matmul_mx(
+                    out=a[:],
+                    lhsT=codes[b][:, tb * P : (tb + 1) * P].bitcast(E5M2X4),
+                    lhsT_scale=hsc[b][:, tb * P : (tb + 1) * P],
+                    rhs=wwords[:, cb * 1024 : (cb + 1) * 1024].bitcast(E2M1X4),
+                    rhs_scale=wplane[:, cb * 512 : (cb + 1) * 512],
+                    start=True,
+                    stop=True,
+                )
 
         def ev(j):
             if not 0 <= j < NT:
@@ -427,7 +429,7 @@ def tile_attentivestatspool_pb_kernel(tc, h, x, mask, w2_words, w2_scales, b2, g
                     new_hil(b)
                 interleave(b, k, "s")
             tr(ta + 2)
-            mx(j0 + 5)
+            mx(j0 + 5, 2)
             if pe_before:
                 fold_sum(v - 1, 0, v - 1)
                 fold_sum(v - 1, 1, 16 + v - 1)

@@ -205,7 +205,7 @@ def tile_attentivestatspool_pb_kernel(tc, h, x, mask, w2_words, w2_scales, b2, g
                 nt = namp.tile([P, 4, 512], F32, name="nam")
                 nam[g] = nt
             col = b * 4 + tb
-            if j in (1, 3, 5):
+            if j in (1, 3, 5, 6):
                 nc.vector.tensor_scalar(
                     out=nam[g][:, tb, :], in0=pa[j][:], scalar1=-1.0, scalar2=pb[:, col : col + 1],
                     op0=ALU.mult, op1=ALU.add,

@@ -350,25 +350,25 @@ def tile_attentivestatspool_pb_kernel(tc, h, x, mask, w2_words, w2_scales, b2, g
         ev(5)
         tr(0)
         tr(1)
+        tr(2)
         mx(6)
         mx(7)
-        tr(2)
-        mx(8)
-        xp(1)
         mn(0)
         ex(0)
         tr(3)
+        mx(8)
+        xp(1)
         mn(1)
         ex(1)
         ev(6)
         ev(7)
+        mx(9)
         mn(2)
         ex(2)
-        ev(8)
         tr(4)
-        tr(5)
-        mx(9)
         mx(10)
+        ev(8)
+        tr(5)
         mx(11)
 
         for v in range(NR):

@@ -205,7 +205,7 @@ def tile_attentivestatspool_pb_kernel(tc, h, x, mask, w2_words, w2_scales, b2, g
                 nt = namp.tile([P, 4, 512], F32, name="nam")
                 nam[g] = nt
             col = b * 4 + tb
-            if j in (1, 3, 5, 6):
+            if j in (1, 3, 6):
                 nc.vector.tensor_scalar(
                     out=nam[g][:, tb, :], in0=pa[j][:], scalar1=-1.0, scalar2=pb[:, col : col + 1],
                     op0=ALU.mult, op1=ALU.add,
@@ -423,8 +423,8 @@ def tile_attentivestatspool_pb_kernel(tc, h, x, mask, w2_words, w2_scales, b2, g
             if two and not by_pe:
                 sum1_scalar(a + 2)
             ev(j0 + 2)
-            if v < 6:
-                b, k = (2, 2 + v) if v < 2 else (3, v - 2)
+            if 1 <= v < 7:
+                b, k = (2, 1 + v) if v < 3 else (3, v - 3)
                 if k == 0:
                     new_hil(b)
                 interleave(b, k, "s")

@@ -416,20 +416,22 @@ def tile_attentivestatspool_pb_kernel(tc, h, x, mask, w2_words, w2_scales, b2, g
                 sum1_scalar(a)
             if last:
                 sum2_scalar(a, pq_last)
-            if pe_before:
+            if pe_before and not by_pe:
                 fold_out(v - 1, 2)
             mn(na + 2)
+            ev(j0 + 2)
+            mx(j0 + 5, 2)
             ex(na + 2)
             if two and not by_pe:
                 sum1_scalar(a + 2)
-            ev(j0 + 2)
+            if pe_before and by_pe:
+                fold_out(v - 1, 2)
             if 1 <= v < 7:
                 b, k = (2, 1 + v) if v < 3 else (3, v - 3)
                 if k == 0:
                     new_hil(b)
                 interleave(b, k, "s")
             tr(ta + 2)
-            mx(j0 + 5, 2)
             if pe_before:
                 fold_sum(v - 1, 0, v - 1)
                 fold_sum(v - 1, 1, 16 + v - 1)

@@ -178,7 +178,7 @@ def tile_attentivestatspool_pb_kernel(tc, h, x, mask, w2_words, w2_scales, b2, g
         pt = {}
 
         def mx(j, times=1):
-            if j < 0:
+            if not 0 <= j < NT:
                 return
             g, tb = divmod(min(j, NT - 1), 4)
             b, cb = divmod(g, NCB)
@@ -420,7 +420,7 @@ def tile_attentivestatspool_pb_kernel(tc, h, x, mask, w2_words, w2_scales, b2, g
                 fold_out(v - 1, 2)
             mn(na + 2)
             ev(j0 + 2)
-            mx(j0 + 5, 2)
+            mx(j0 + 5)
             ex(na + 2)
             if two and not by_pe:
                 sum1_scalar(a + 2)

from contextlib import ExitStack

import concourse.mybir as mybir
from concourse.masks import make_identity

B, C, T, H = 4, 1536, 512, 512
FLOPS = 2 * B * C * H * T

F32 = mybir.dt.float32
BF16 = mybir.dt.bfloat16
U32 = mybir.dt.uint32
U8 = mybir.dt.uint8
I32 = mybir.dt.int32
E5M2X4 = mybir.dt.float8_e5m2_x4
E2M1X4 = mybir.dt.float4_e2m1fn_x4
ACT = mybir.ActivationFunctionType
ALU = mybir.AluOpType
AX = mybir.AxisListType

P = 128
NCB = C // 512
NG = B * NCB
NT = NG * 4
JT = C // P
NR = NT // 3
BIG = 2.0 ** 100
EPS_STD = 1e-5
EPS_LN = 1e-5


def tile_attentivestatspool_pb_kernel(tc, h, x, mask, w2_words, w2_scales, b2, g2, be2, out):
    nc = tc.nc
    with ExitStack() as ctx:
        const = ctx.enter_context(tc.tile_pool(name="const", bufs=1))
        hilp = ctx.enter_context(tc.tile_pool(name="hilp", bufs=2))
        namp = ctx.enter_context(tc.tile_pool(name="namp", bufs=3))
        ep = ctx.enter_context(tc.tile_pool(name="ep", bufs=7))
        pp = ctx.enter_context(tc.tile_pool(name="pp", bufs=3))
        gp = ctx.enter_context(tc.tile_pool(name="gp", bufs=2))
        psa = ctx.enter_context(tc.psum_pool(name="psa", bufs=3))
        psb = ctx.enter_context(tc.psum_pool(name="psb", bufs=3))
        psf = ctx.enter_context(tc.psum_pool(name="psf", bufs=1))
        fp = ctx.enter_context(tc.tile_pool(name="fp", bufs=2))
        psm = ctx.enter_context(tc.psum_pool(name="psm", bufs=1))
        ctx.enter_context(tc.manual_schedule())

        hraw = []
        codes = []
        hsc = []
        for b in range(B):
            hr = const.tile([P, 4, T], BF16, name="hraw%d" % b)
            cd = const.tile([P, T], U32, name="codes%d" % b, align_bytes=64)
            sc = const.tile([P, T], U8, name="hsc%d" % b, align_bytes=64)
            hraw.append(hr)
            codes.append(cd)
            hsc.append(sc)
        xs = []
        for g in range(NG):
            xt = const.tile([P, 4, T], BF16, name="x%d" % g)
            xs.append(xt)
        wwords = const.tile([P, 2 * C], U8, name="wwords", align_bytes=64)
        wplane = const.tile([P, C], U8, name="wplane", align_bytes=64)
        mrow = const.tile([P, P], BF16, name="mrow")
        pbrow = const.tile([P, P], F32, name="pbrow")
        pb = const.tile([P, 16], F32, name="pb")
        ident = const.tile([P, P], F32, name="ident")
        identb = const.tile([P, P], BF16, name="identb")
        ones = const.tile([P, P], F32, name="ones")
        ysel = const.tile([P, P], F32, name="ysel")
        oh = const.tile([P, B], F32, name="oh")
        warm = const.tile([P, 1], F32, name="warm")
        warm2 = const.tile([P, 1], F32, name="warm2")
        epst = const.tile([P, 1], F32, name="epst")
        s0 = const.tile([P, NT], F32, name="s0")
        s1 = const.tile([P, NT], F32, name="s1")
        s2 = const.tile([P, NT], F32, name="s2")
        negm = const.tile([P, NT], F32, name="negm")
        vt = const.tile([P, P], F32, name="vt")
        g2t = const.tile([P, P], BF16, name="g2t")
        be2t = const.tile([P, P], BF16, name="be2t")

        def load_h(b):
            nc.sync.dma_start(out=hraw[b][:], in_=h[b].rearrange("(p j) t -> p j t", j=4))

        def load_x(g):
            b, cb = divmod(g, NCB)
            nc.sync.dma_start(
                out=xs[g][:],
                in_=x[b, cb * 512 : (cb + 1) * 512, :].rearrange("(cc p) t -> p cc t", p=P),
            )

        load_h(0)
        nc.gpsimd.memset(mrow[:], 0.0)
        nc.scalar.dma_start(out=mrow[0:16, :], in_=mask.rearrange("b o (tb p) -> (b o tb) p", p=P))
        nc.vector.memset(wplane[:].bitcast(I32), 0)
        nc.vector.memset(ysel[:], 0.0)
        for b in range(B):
            nc.vector.memset(ysel[32 * b : 32 * (b + 1), 24 * b : 24 * (b + 1)], 1.0)
        nc.vector.memset(ones[:], 1.0)
        nc.vector.memset(vt[:], 0.0)
        nc.vector.memset(epst[:], EPS_LN)
        for q in range(4):
            nc.sync.dma_start(
                out=wplane[32 * q : 32 * q + 4, :].bitcast(I32),
                in_=w2_scales[0, 4 * q : 4 * q + 4, :].bitcast(I32),
            )
        nc.sync.dma_start(out=wwords[:].bitcast(I32), in_=w2_words[0].bitcast(I32))
        load_h(1)
        load_x(0)
        load_h(2)
        load_x(1)
        load_x(2)
        load_h(3)
        for g in range(NCB, NG):
            load_x(g)
        for b in range(B):
            nc.sync.dma_start(out=g2t[b * 24 : (b + 1) * 24, :], in_=g2.rearrange("(j p) -> j p", p=P))
            nc.sync.dma_start(out=be2t[b * 24 : (b + 1) * 24, :], in_=be2.rearrange("(j p) -> j p", p=P))

        make_identity(nc, ident[:])
        nc.gpsimd.memset(warm[:], 1.0)
        make_identity(nc, identb[:])
        nc.scalar.activation(out=warm2[:], in_=warm[:], func=ACT.Exp)

        pbt = psm.tile([P, 512], F32, name="pbt", tag="misc")
        nc.tensor.transpose(pbt[:, P : 2 * P], ysel[:], ident[:])
        nc.vector.tensor_copy(out=oh[:], in_=pbt[:, P : 2 * P : 32])
        nc.vector.tensor_scalar(out=pbrow[:], in0=mrow[:], scalar1=-BIG, scalar2=BIG, op0=ALU.mult, op1=ALU.add)
        nc.tensor.transpose(pbt[:, 0:P], pbrow[:], ident[:])
        nc.scalar.copy(out=pb[:], in_=pbt[:, 0:16])

        hil = {}

        def new_hil(b):
            hl = hilp.tile([P, T, 4], BF16, name="hil", align_bytes=64)
            hil[b] = hl

        def interleave(b, k, eng):
            dst = hil[b][:, k * P : (k + 1) * P, :]
            src = hraw[b][:, :, k * P : (k + 1) * P].rearrange("p j t -> p t j")
            if eng != "g":
                dst = hil[b][:, k * P : (k + 1) * P, :].rearrange("p (c i) j -> p c j i", i=4)
                src = hraw[b][:, :, k * P : (k + 1) * P].rearrange("p j (c i) -> p c j i", i=4)
            if eng == "v":
                nc.vector.tensor_copy(out=dst, in_=src)
            elif eng == "s":
                nc.scalar.copy(out=dst, in_=src)
            else:
                nc.gpsimd.tensor_scalar(out=dst, in0=src, scalar1=1.0, scalar2=0.0, op0=ALU.mult, op1=ALU.add)

        def quantize(b, lo, hi):
            nc.vector.quantize_mx(
                out=codes[b][:, lo:hi].bitcast(E5M2X4),
                scales=hsc[b][:, lo:hi],
                in_=hil[b][:, lo:hi, :].rearrange("p t j -> p (t j)"),
            )

        new_hil(0)
        interleave(0, 0, "v")
        interleave(0, 1, "v")
        interleave(0, 2, "s")
        interleave(0, 3, "s")
        for k in range(4):
            quantize(0, k * P, (k + 1) * P)
        new_hil(1)
        nc.gpsimd.tensor_scalar(
            out=hil[1][:], in0=hraw[1][:].rearrange("p j t -> p t j"), scalar1=1.0, scalar2=0.0,
            op0=ALU.mult, op1=ALU.add,
        )
        new_hil(2)
        interleave(2, 0, "g")
        interleave(2, 1, "g")

        pa = {}
        nam = {}
        pbk = {}
        et = {}
        pt = {}

        def mx(j, times=1):
            if not 0 <= j < NT:
                return
            g, tb = divmod(min(j, NT - 1), 4)
            b, cb = divmod(g, NCB)
            a = psa.tile([P, 512], F32, name="psA")
            if j < NT:
                pa[j] = a
            for rpt in range(times):
                nc.tensor.matmul_mx(
                    out=a[:],
                    lhsT=codes[b][:, tb * P : (tb + 1) * P].bitcast(E5M2X4),
                    lhsT_scale=hsc[b][:, tb * P : (tb + 1) * P],
                    rhs=wwords[:, cb * 1024 : (cb + 1) * 1024].bitcast(E2M1X4),
                    rhs_scale=wplane[:, cb * 512 : (cb + 1) * 512],
                    start=True,
                    stop=True,
                )

        def ev(j):
            if not 0 <= j < NT:
                return
            g, tb = divmod(j, 4)
            b = g // NCB
            if tb == 0:
                nt = namp.tile([P, 4, 512], F32, name="nam")
                nam[g] = nt
            col = b * 4 + tb
            if j in (1, 3, 6):
                nc.vector.tensor_scalar(
                    out=nam[g][:, tb, :], in0=pa[j][:], scalar1=-1.0, scalar2=pb[:, col : col + 1],
                    op0=ALU.mult, op1=ALU.add,
                )
            else:
                nc.scalar.activation(
                    out=nam[g][:, tb, :], in_=pa[j][:], func=ACT.Identity, bias=pb[:, col : col + 1], scale=-1.0
                )

        def tr(i):
            if not 0 <= i < NT:
                return
            g, cc = divmod(i, 4)
            bk = psb.tile([P, 512], F32, name="psB")
            pbk[i] = bk
            for tb in range(4):
                nc.tensor.transpose(bk[:, tb * P : (tb + 1) * P], nam[g][:, tb, cc * P : (cc + 1) * P], ident[:])

        def mn(i):
            if not 0 <= i < NT:
                return
            nc.vector.tensor_reduce(out=negm[:, i : i + 1], in_=pbk[i][:], axis=AX.X, op=ALU.min)

        def ex(i):
            if not 0 <= i < NT:
                return
            e = ep.tile([P, 512], F32, name="e")
            et[i] = e
            nc.scalar.activation(
                out=e[:], in_=pbk[i][:], func=ACT.Exp, bias=negm[:, i : i + 1], scale=-1.0,
                accum_out=s0[:, i : i + 1],
            )
            if i == NT - 1:
                nc.scalar.activation(out=warm2[:], in_=warm[:], func=ACT.Sqrt)

        def xtile(i):
            g, cc = divmod(i, 4)
            return xs[g][:, cc, :]

        xpt = {}
        pgt = {}

        def xp(i):
            if not 0 <= i < NT:
                return
            xq = psm.tile([P, 512], F32, name="xq", tag="misc")
            xpt[i] = xq
            nc.tensor.matmul(out=xq[:], lhsT=identb[:], rhs=xtile(i), start=True, stop=True)

        def xin(i):
            if i in xpt:
                return xpt[i][:]
            return xtile(i)

        def prod1(i):
            p1 = pp.tile([P, 512], F32, name="p1")
            pt[i] = p1
            nc.vector.scalar_tensor_tensor(
                out=p1[:], in0=et[i][:], scalar=1.0, in1=xin(i), op0=ALU.mult, op1=ALU.mult,
                accum_out=s1[:, i : i + 1],
            )

        def new_pg(i):
            pg = gp.tile([P, 512], F32, name="pg")
            pgt[i] = pg
            pt[i] = pg

        def new_pg2(i):
            pg2 = gp.tile([P, 512], F32, name="pg2")
            pt[i] = pg2

        def prod1_gpsimd(i):
            nc.gpsimd.tensor_tensor(out=pt[i][:], in0=et[i][:], in1=xtile(i), op=ALU.mult)

        def sum1_scalar(i):
            sj = gp.tile([P, 512], BF16, name="sj")
            nc.scalar.activation(out=sj[:], in_=pt[i][:], func=ACT.Identity, accum_out=s1[:, i : i + 1])

        fs = psf.tile([P, 512], F32, name="fs")
        fsb = {}

        def fold(i, region):
            for tb in range(4):
                nc.tensor.matmul(
                    out=fs[:, region * P : (region + 1) * P], lhsT=pt[i][:, tb * P : (tb + 1) * P], rhs=ident[:],
                    is_transpose=True, start=(tb == 0), stop=(tb == 3),
                )

        def fold_out(v, regions):
            fb = fp.tile([P, 3 * P], F32, name="fb")
            fsb[v] = fb
            nc.scalar.copy(out=fb[:, 0 : regions * P], in_=fs[:, 0 : regions * P])

        def fold_sum(v, region, col):
            nc.tensor.matmul(
                out=fs[:, 3 * P + col : 3 * P + col + 1], lhsT=fsb[v][:, region * P : (region + 1) * P],
                rhs=ones[:, 0:1], start=True, stop=True,
            )

        def xp_spare(i):
            xq = psa.tile([P, 512], F32, name="psA")
            xpt[i] = xq
            nc.tensor.matmul(out=xq[:], lhsT=identb[:], rhs=xtile(i), start=True, stop=True)

        def prod2_gpsimd(i):
            pq = gp.tile([P, 512], F32, name="pq")
            nc.gpsimd.tensor_tensor(out=pq[:], in0=pt[i][:], in1=xtile(i), op=ALU.mult)
            return pq

        def sum2_scalar(i, pq):
            sj = gp.tile([P, 512], BF16, name="sj")
            nc.scalar.activation(out=sj[:], in_=pq[:], func=ACT.Identity, accum_out=s2[:, i : i + 1])

        def prod2(i, junk):
            nc.vector.scalar_tensor_tensor(
                out=junk[:], in0=pt[i][:], scalar=1.0, in1=xin(i), op0=ALU.mult, op1=ALU.mult,
                accum_out=s2[:, i : i + 1],
            )

        def new_junk():
            p2 = pp.tile([P, 512], F32, name="p2")
            return p2

        def v3(ap):
            return ap.rearrange("p (b j) -> p b j", b=B)

        vt3 = v3(vt[:, 0 : 2 * NT])
        r0 = const.tile([P, NT], F32, name="r0")
        msq = const.tile([P, NT], F32, name="msq")

        mx(0)
        mx(1)
        mx(2)
        ev(0)
        ev(1)
        mx(3)
        mx(4)
        ev(2)
        mx(5)
        ev(3)
        ev(4)
        ev(5)
        tr(0)
        tr(1)
        tr(2)
        mx(6)
        mx(7)
        mn(0)
        ex(0)
        tr(3)
        mx(8)
        xp(1)
        mn(1)
        ex(1)
        ev(6)
        ev(7)
        mx(9)
        mn(2)
        ex(2)
        tr(4)
        mx(10)
        ev(8)
        tr(5)
        mx(11)

        for v in range(NR):
            a = 3 * v
            na = a + 3
            ta = a + 6
            j0 = a + 9
            helped = v < NR - 1
            two = helped
            last = v == NR - 1
            by_pe = v < NR - 2
            pe_before = 1 <= v < NR - 1
            ev(j0)
            mn(na)
            if v == 0:
                quantize(1, 0, T)
            if a not in pgt:
                new_pg(a)
            prod1_gpsimd(a)
            if last:
                xp_spare(a + 2)
                pq_last = prod2_gpsimd(a)
            if two:
                new_pg2(a + 2)
                prod1_gpsimd(a + 2)
            prod1(a + 1)
            if last:
                nc.vector.reciprocal(out=r0[:], in_=s0[:])
                npe = NR - 2
                nc.vector.tensor_copy(out=s1[:, 0 : 3 * npe : 3], in_=fs[:, 3 * P : 3 * P + npe])
                nc.vector.tensor_copy(out=s1[:, 2 : 3 * npe : 3], in_=fs[:, 3 * P + 16 : 3 * P + 16 + npe])
            ex(na)
            tr(ta)
            ev(j0 + 1)
            mn(na + 1)
            mx(j0 + 3)
            mx(j0 + 4)
            if last:
                prod1(a + 2)
            prod2(a + 1, new_junk())
            xp(a + 4)
            ex(na + 1)
            tr(ta + 1)
            if not by_pe:
                sum1_scalar(a)
            if last:
                sum2_scalar(a, pq_last)
            if pe_before and not by_pe:
                fold_out(v - 1, 2)
            mn(na + 2)
            ev(j0 + 2)
            mx(j0 + 5)
            ex(na + 2)
            if two and not by_pe:
                sum1_scalar(a + 2)
            if pe_before and by_pe:
                fold_out(v - 1, 2)
            if 1 <= v < 7:
                b, k = (2, 1 + v) if v < 3 else (3, v - 3)
                if k == 0:
                    new_hil(b)
                interleave(b, k, "s")
            tr(ta + 2)
            if pe_before:
                fold_sum(v - 1, 0, v - 1)
                fold_sum(v - 1, 1, 16 + v - 1)
            if by_pe:
                fold(a, 0)
                fold(a + 2, 1)
            if last:
                prod2(a + 2, new_junk())
                nc.vector.tensor_tensor(out=vt3[:, :, 0:JT], in0=v3(s1[:]), in1=v3(r0[:]), op=ALU.mult)
                nc.vector.tensor_tensor(out=v3(msq[:]), in0=vt3[:, :, 0:JT], in1=vt3[:, :, 0:JT], op=ALU.mult)
            else:
                if not two:
                    prod1(a + 2)
                for b in range(2, B):
                    if v == 4 * b - 5:
                        quantize(b, 0, T)
                new_pg(a + 3)
                prod2(a, pgt[a + 3])
                prod2(a + 2, new_junk())

        ex2 = const.tile([P, NT], F32, name="ex2")
        t2 = const.tile([P, NT], F32, name="t2")
        var = const.tile([P, NT], F32, name="var")
        st = const.tile([P, 2 * B], F32, name="st")
        mom = const.tile([P, 2], F32, name="mom")
        nv = const.tile([P, 1], F32, name="nv")
        sd = const.tile([P, 1], F32, name="sd")
        rstd = const.tile([P, 1], F32, name="rstd")
        o1 = const.tile([P, P], F32, name="o1")
        o2 = const.tile([P, P], F32, name="o2")
        mj = const.tile([P, 2 * B], F32, name="mj")
        R = 2 * JT * B

        nc.vector.tensor_tensor(out=ex2[:], in0=s2[:], in1=r0[:], op=ALU.mult)
        nc.vector.scalar_tensor_tensor(
            out=t2[:], in0=msq[:], scalar=EPS_STD, in1=ex2[:], op0=ALU.add, op1=ALU.max
        )
        nc.vector.tensor_tensor(out=var[:], in0=t2[:], in1=msq[:], op=ALU.subtract)
        nc.scalar.activation(out=vt3[:, :, JT : 2 * JT], in_=v3(var[:]), func=ACT.Sqrt)
        nc.vector.tensor_reduce(out=st[:, B : 2 * B], in_=v3(t2[:]), axis=AX.X, op=ALU.add)
        nc.vector.tensor_reduce(out=st[:, 0:B], in_=vt3, axis=AX.X, op=ALU.add)
        fin = psm.tile([P, 512], F32, name="fin", tag="misc")
        nc.tensor.transpose(fin[:, 0:P], vt[:], ident[:])
        nc.tensor.matmul(out=fin[:, P : P + 2 * B], lhsT=ones[:], rhs=st[:], start=True, stop=True)
        for k in range(2):
            nc.vector.scalar_tensor_tensor(
                out=mj[:, k * B : (k + 1) * B], in0=fin[:, P + k * B : P + (k + 1) * B], scalar=1.0 / (2 * C),
                in1=oh[:], op0=ALU.mult, op1=ALU.mult, accum_out=mom[:, k : k + 1],
            )
        nc.vector.scalar_tensor_tensor(
            out=nv[:], in0=mom[:, 0:1], scalar=mom[:, 0:1], in1=mom[:, 1:2], op0=ALU.mult, op1=ALU.subtract
        )
        nc.scalar.activation(out=sd[:], in_=nv[:], func=ACT.Sqrt, bias=epst[:, 0:1], scale=-1.0)
        nc.vector.scalar_tensor_tensor(
            out=o1[0:R, :], in0=fin[0:R, 0:P], scalar=mom[0:R, 0:1], in1=g2t[0:R, :], op0=ALU.subtract, op1=ALU.mult
        )
        nc.vector.reciprocal(out=rstd[:], in_=sd[:])
        nc.vector.scalar_tensor_tensor(
            out=o2[0:R, :], in0=o1[0:R, :], scalar=rstd[0:R, 0:1], in1=be2t[0:R, :], op0=ALU.mult, op1=ALU.add
        )
        outr = out.rearrange("b (j p) o -> (b j) (p o)", p=P)
        nc.sync.dma_start(out=outr[0:64, :], in_=o2[0:64, :])
        nc.scalar.dma_start(out=outr[64:R, :], in_=o2[64:R, :])
